import numpy as np
import ml_dtypes


def mxq(x, axis, fmt="e4m3"):
    dtype, down = {"e4m3": (ml_dtypes.float8_e4m3fn, 7), "e5m2": (ml_dtypes.float8_e5m2, 14)}[fmt]
    v = np.moveaxis(np.asarray(x, np.float32).astype(ml_dtypes.bfloat16).astype(np.float64), axis, -1)
    blocks = v.reshape(v.shape[:-1] + (-1, 32))
    amax = np.abs(blocks).max(-1, keepdims=True)
    byte = np.maximum(np.where(amax > 0, np.frexp(amax)[1] - 1 + 127, 0) - down, 1)
    scale = np.exp2(byte - 127.0)
    codes = (blocks / scale).astype(np.float32).astype(dtype).astype(np.float64)
    return np.moveaxis((codes * scale).reshape(v.shape), -1, axis)


WIDE = False


def mx_kscale(k):
    if not WIDE:
        return np.ones(k)
    levels = np.array([10, -10, 5, -5, 0])
    a = np.random.permutation(np.resize(levels, k // 512 * 4)).reshape(k // 512, 4)
    idx = np.arange(k)
    return np.exp2(a[idx // 512, idx % 128 // 32])


BF16 = ml_dtypes.bfloat16


def bf(x):
    return np.asarray(x, np.float32).astype(BF16)


def f64(x):
    return np.asarray(x).astype(np.float64)


E2M1 = np.array([0.0, 0.5, 1.0, 1.5, 2.0, 3.0, 4.0, 6.0, -0.0, -0.5, -1.0, -1.5, -2.0, -3.0, -4.0, -6.0])


def pack_weight(w, fmt):
    k, n = w.shape
    w = f64(bf(w)).reshape(k // 32, 32, n)
    amax = np.abs(w).max(1)
    if fmt == "e4m3":
        byte = np.frexp(amax)[1] - 1 + 127 - 7
    else:
        mant, ex = np.frexp(amax / 6.0)
        byte = np.where(mant > 0.5, ex, ex - 1) + 127
    byte = np.clip(np.where(amax > 0, byte, 1), 1, 254)
    scaled = (w * np.exp2(127.0 - byte)[:, None, :]).reshape(k, n).astype(np.float32)
    by_word = np.ascontiguousarray(scaled.reshape(k // 512, 128, 4, n).transpose(0, 1, 3, 2))
    if fmt == "e4m3":
        words = by_word.astype(ml_dtypes.float8_e4m3fn).view(np.uint8)
    else:
        c = by_word.astype(ml_dtypes.float4_e2m1fn).view(np.uint8) & 0xF
        words = c[..., 0::2] | (c[..., 1::2] << 4)
    return np.ascontiguousarray(words), np.ascontiguousarray(byte.astype(np.uint8).reshape(k // 512, 16, n))


def unpack_weight(words, scales, fmt):
    g, p, n, _ = words.shape
    if fmt == "e4m3":
        vals = np.ascontiguousarray(words).view(ml_dtypes.float8_e4m3fn).astype(np.float64)
    else:
        nib = np.empty((g, p, n, 4), np.uint8)
        nib[..., 0::2] = words & 0xF
        nib[..., 1::2] = words >> 4
        vals = E2M1[nib]
    vals = vals * np.repeat(np.exp2(scales.astype(np.float64) - 127.0), 8, axis=1)[..., None]
    return vals.transpose(0, 1, 3, 2).reshape(g * 512, n)


B, D_IN, D_OUT = 4096, 512, 512
FMT = "e4m3"


def sigmoid(v):
    return 1.0 / (1.0 + np.exp(-v))


def setup_inputs():
    s, t = mx_kscale(D_IN), mx_kscale(D_OUT)

    def wx():
        return pack_weight(np.random.standard_normal((D_IN, D_OUT)) / np.sqrt(D_IN) / s[:, None], FMT)

    def wh():
        return pack_weight(np.random.standard_normal((D_OUT, D_OUT)) / np.sqrt(D_OUT) / t[:, None], FMT)

    x = bf(np.random.standard_normal((B, D_IN)) * s)
    hist = bf(np.random.standard_normal((B, D_OUT)) * t)
    ig = bf(np.random.standard_normal((B, D_OUT)) * 0.4)
    carousel = bf(np.random.uniform(1.25, 1.75, 1))
    Wfx_words, Wfx_scales = wx()
    Wfh_words, Wfh_scales = wh()
    b_f = bf(np.random.standard_normal(D_OUT) * 0.3)
    Wox_words, Wox_scales = wx()
    Woh_words, Woh_scales = wh()
    b_o = bf(np.random.standard_normal(D_OUT) * 0.3)
    return {"x": x,
            "hist": hist,
            "ig": ig,
            "carousel": carousel,
            "Wfx_words": Wfx_words, "Wfx_scales": Wfx_scales,
            "Wfh_words": Wfh_words, "Wfh_scales": Wfh_scales,
            "b_f": b_f,
            "Wox_words": Wox_words, "Wox_scales": Wox_scales,
            "Woh_words": Woh_words, "Woh_scales": Woh_scales,
            "b_o": b_o}


def reference(x, hist, ig, carousel, Wfx_words, Wfx_scales, Wfh_words, Wfh_scales, b_f, Wox_words, Wox_scales, Woh_words, Woh_scales, b_o):
    xq = mxq(f64(x), 1, "e4m3")
    hq = mxq(f64(hist), 1, "e4m3")
    f = sigmoid((xq @ unpack_weight(Wfx_words, Wfx_scales, FMT)) + (hq @ unpack_weight(Wfh_words, Wfh_scales, FMT)) + f64(b_f))
    o = sigmoid((xq @ unpack_weight(Wox_words, Wox_scales, FMT)) + (hq @ unpack_weight(Woh_words, Woh_scales, FMT)) + f64(b_o))
    c = f * f64(carousel) + f64(ig)
    h = o * c
    return (h, c)

@@ -1,0 +1,212 @@
+from contextlib import ExitStack
+
+import concourse.mybir as mybir
+from concourse.masks import make_identity
+
+F32 = mybir.dt.float32
+BF16 = mybir.dt.bfloat16
+I32 = mybir.dt.int32
+U32 = mybir.dt.uint32
+U8 = mybir.dt.uint8
+FP8X4 = mybir.dt.float8_e4m3fn_x4
+ADD = mybir.AluOpType.add
+MULT = mybir.AluOpType.mult
+SIGMOID = mybir.ActivationFunctionType.Sigmoid
+
+P = 128
+BATCH = 4096
+D = 512
+PACK = 4
+ROW_TILES = BATCH // P
+ROUND_TILES = 2
+ROUNDS = ROW_TILES // ROUND_TILES
+CHUNK_TILES = 4
+CHUNKS = ROW_TILES // CHUNK_TILES
+GATES = 2
+SOURCES = 2
+OUT_BUFS = 8
+
+FLOPS = 2 * BATCH * D * D * GATES * SOURCES
+
+
+def tile_lstmmirrored_pb_t_kernel(
+    tc,
+    x,
+    hist,
+    ig,
+    carousel,
+    Wfx_words,
+    Wfx_scales,
+    Wfh_words,
+    Wfh_scales,
+    b_f,
+    Wox_words,
+    Wox_scales,
+    Woh_words,
+    Woh_scales,
+    b_o,
+    out_0,
+    out_1,
+):
+    nc = tc.nc
+
+    x_rows = x.rearrange("(p t) d -> p t d", t=ROW_TILES)
+    hist_rows = hist.rearrange("(p t) d -> p t d", t=ROW_TILES)
+    ig_rows = ig.rearrange("(p t) d -> p t d", t=ROW_TILES)
+    h_rows = out_0.rearrange("(p t) d -> p t d", t=ROW_TILES)
+    c_rows = out_1.rearrange("(p t) d -> p t d", t=ROW_TILES)
+
+    weight_words = [Wfx_words, Wfh_words, Wox_words, Woh_words]
+    weight_scales = [Wfx_scales, Wfh_scales, Wox_scales, Woh_scales]
+
+    with ExitStack() as stack:
+        const = stack.enter_context(tc.tile_pool(name="const", bufs=1))
+        inputs = stack.enter_context(tc.tile_pool(name="inputs", bufs=1))
+        quant = stack.enter_context(tc.tile_pool(name="quant", bufs=3))
+        gates = stack.enter_context(tc.tile_pool(name="gates", bufs=3))
+        results = stack.enter_context(tc.tile_pool(name="results", bufs=OUT_BUFS))
+        psum_t = stack.enter_context(tc.psum_pool(name="psum_t", bufs=2))
+        psum_mx = stack.enter_context(tc.psum_pool(name="psum_mx", bufs=6))
+        stack.enter_context(tc.manual_schedule())
+
+        w_words = const.tile([P, GATES * SOURCES, D], U32, align_bytes=64)
+        w_planes = const.tile([P, GATES * SOURCES, D], U8, align_bytes=64)
+        bias = const.tile([P, GATES, D], BF16)
+        gain_bf = const.tile([P, 1], BF16)
+        gain = const.tile([P, 1], F32)
+        table_warm = const.tile([P, 1], F32)
+        identity = const.tile([P, P], F32)
+
+        nc.vector.memset(w_planes[:].rearrange("p w n -> p (w n)").bitcast(I32), 0)
+        nc.vector.memset(table_warm[:], 0.0)
+        make_identity(nc, identity[:])
+
+        x_chunks = []
+        hist_chunks = []
+        ig_chunks = []
+        for chunk in range(CHUNKS):
+            x_chunk = inputs.tile([P, CHUNK_TILES, D], BF16, name="x%d" % chunk)
+            hist_chunk = inputs.tile([P, CHUNK_TILES, D], BF16, name="hist%d" % chunk)
+            ig_chunk = inputs.tile([P, CHUNK_TILES, D], BF16, name="ig%d" % chunk)
+            x_chunks.append(x_chunk)
+            hist_chunks.append(hist_chunk)
+            ig_chunks.append(ig_chunk)
+
+        def chunk_rows(chunk):
+            return slice(chunk * CHUNK_TILES, (chunk + 1) * CHUNK_TILES)
+
+        nc.scalar.dma_start(out=x_chunks[0][:], in_=x_rows[:, chunk_rows(0), :])
+        nc.scalar.dma_start(out=hist_chunks[0][:], in_=hist_rows[:, chunk_rows(0), :])
+        nc.scalar.dma_start(out=gain_bf[:], in_=carousel.partition_broadcast(P))
+        nc.scalar.dma_start(out=bias[:, 0, :], in_=b_f.partition_broadcast(P))
+        nc.scalar.dma_start(out=bias[:, 1, :], in_=b_o.partition_broadcast(P))
+        nc.scalar.activation(out=table_warm[:], in_=table_warm[:], func=SIGMOID)
+
+        for w in range(GATES * SOURCES):
+            for r in range(4):
+                nc.sync.dma_start(
+                    out=w_planes[r:P:32, w, :].bitcast(I32),
+                    in_=weight_scales[w][0, r:16:4, :].bitcast(I32),
+                )
+        for w in range(GATES * SOURCES):
+            nc.sync.dma_start(
+                out=w_words[:, w, :].bitcast(I32),
+                in_=weight_words[w][0].rearrange("p n t -> p (n t)").bitcast(I32),
+            )
+        nc.sync.dma_start(out=ig_chunks[0][:], in_=ig_rows[:, chunk_rows(0), :])
+        for chunk in range(1, CHUNKS):
+            nc.sync.dma_start(out=x_chunks[chunk][:], in_=x_rows[:, chunk_rows(chunk), :])
+            nc.sync.dma_start(out=hist_chunks[chunk][:], in_=hist_rows[:, chunk_rows(chunk), :])
+            nc.sync.dma_start(out=ig_chunks[chunk][:], in_=ig_rows[:, chunk_rows(chunk), :])
+
+        grouped_of = {}
+        codes_of = {}
+        planes_of = {}
+        gates_of = {}
+
+        def transpose_and_regroup(rnd):
+            grouped = quant.tile([P, ROUND_TILES, SOURCES * P * PACK], BF16, align_bytes=64)
+            grouped_of[rnd] = grouped
+            for j in range(ROUND_TILES):
+                t = rnd * ROUND_TILES + j
+                xt = psum_t.tile([P, 2, SOURCES, P], F32)
+                for source, chunks in enumerate((x_chunks, hist_chunks)):
+                    words = chunks[t // CHUNK_TILES][:, t % CHUNK_TILES, :].bitcast(F32)
+                    for u in range(2):
+                        nc.tensor.transpose(xt[:, u, source, :], words[:, u : D // 2 : 2], identity[:])
+                nc.scalar.copy(
+                    out=grouped[:, j, :].bitcast(F32).rearrange("p (c u) -> p c u", u=2),
+                    in_=xt[:].rearrange("p u s r -> p (s r) u"),
+                )
+
+        def quantise(rnd):
+            codes = quant.tile([P, ROUND_TILES * SOURCES * P], U32, align_bytes=64)
+            planes = quant.tile([P, ROUND_TILES * SOURCES * P], U8, align_bytes=64)
+            codes_of[rnd] = codes
+            planes_of[rnd] = planes
+            nc.vector.quantize_mx(
+                out=codes[:].bitcast(FP8X4),
+                scales=planes[:],
+                in_=grouped_of[rnd][:].rearrange("p j c -> p (j c)"),
+            )
+
+        def gate_sums(rnd):
+            pre = gates.tile([P, ROUND_TILES, GATES, D], F32)
+            gates_of[rnd] = pre
+            for j in range(ROUND_TILES):
+                for gate in range(GATES):
+                    acc = psum_mx.tile([P, D], F32)
+                    for source in range(SOURCES):
+                        rows = slice((j * SOURCES + source) * P, (j * SOURCES + source + 1) * P)
+                        w = gate * SOURCES + source
+                        nc.tensor.matmul_mx(
+                            out=acc[:],
+                            lhsT=codes_of[rnd][:, rows].bitcast(FP8X4),
+                            lhsT_scale=planes_of[rnd][:, rows],
+                            rhs=w_words[:, w, :].bitcast(FP8X4),
+                            rhs_scale=w_planes[:, w, :],
+                            start=(source == 0),
+                            stop=(source == SOURCES - 1),
+                        )
+                    nc.vector.tensor_tensor(out=pre[:, j, gate, :], in0=acc[:], in1=bias[:, gate, :], op=ADD)
+
+        def sigmoids(rnd):
+            for j in range(ROUND_TILES):
+                both = gates_of[rnd][:, j, :, :].rearrange("p g d -> p (g d)")
+                nc.scalar.activation(out=both, in_=both, func=SIGMOID)
+
+        def cell_and_hidden(rnd):
+            t = rnd * ROUND_TILES
+            tiles = slice(t, t + ROUND_TILES)
+            in_chunk = slice(t % CHUNK_TILES, t % CHUNK_TILES + ROUND_TILES)
+            c_out = results.tile([P, ROUND_TILES, D], F32)
+            h_out = results.tile([P, ROUND_TILES, D], F32)
+            nc.vector.scalar_tensor_tensor(
+                out=c_out[:],
+                in0=gates_of[rnd][:, :, 0, :],
+                scalar=gain[:],
+                in1=ig_chunks[t // CHUNK_TILES][:, in_chunk, :],
+                op0=MULT,
+                op1=ADD,
+            )
+            nc.sync.dma_start(out=c_rows[:, tiles, :], in_=c_out[:])
+            for j in range(ROUND_TILES):
+                nc.gpsimd.tensor_tensor(
+                    out=h_out[:, j, :], in0=gates_of[rnd][:, j, 1, :], in1=c_out[:, j, :], op=MULT
+                )
+            nc.sync.dma_start(out=h_rows[:, tiles, :], in_=h_out[:])
+
+        transpose_and_regroup(0)
+        quantise(0)
+        nc.vector.tensor_copy(out=gain[:], in_=gain_bf[:])
+        for step in range(ROUNDS + 1):
+            if step + 1 < ROUNDS:
+                transpose_and_regroup(step + 1)
+            if step < ROUNDS:
+                gate_sums(step)
+            if step + 1 < ROUNDS:
+                quantise(step + 1)
+            if step < ROUNDS:
+                sigmoids(step)
+            if step >= 1:
+                cell_and_hidden(step - 1)

@@ -190,10 +190,7 @@ def tile_lstmmirrored_pb_t_kernel(
                 op1=ADD,
             )
             nc.sync.dma_start(out=c_rows[:, tiles, :], in_=c_out[:])
-            for j in range(ROUND_TILES):
-                nc.gpsimd.tensor_tensor(
-                    out=h_out[:, j, :], in0=gates_of[rnd][:, j, 1, :], in1=c_out[:, j, :], op=MULT
-                )
+            nc.vector.tensor_tensor(out=h_out[:], in0=gates_of[rnd][:, :, 1, :], in1=c_out[:], op=MULT)
             nc.sync.dma_start(out=h_rows[:, tiles, :], in_=h_out[:])
 
         transpose_and_regroup(0)

@@ -18,8 +18,8 @@ BATCH = 4096
 D = 512
 PACK = 4
 ROW_TILES = BATCH // P
-ROUND_TILES = 2
-ROUNDS = ROW_TILES // ROUND_TILES
+STORE_TILES = 2
+LEAD = 2
 CHUNK_TILES = 4
 CHUNKS = ROW_TILES // CHUNK_TILES
 GATES = 2
@@ -62,8 +62,8 @@ def tile_lstmmirrored_pb_t_kernel(
     with ExitStack() as stack:
         const = stack.enter_context(tc.tile_pool(name="const", bufs=1))
         inputs = stack.enter_context(tc.tile_pool(name="inputs", bufs=1))
-        quant = stack.enter_context(tc.tile_pool(name="quant", bufs=3))
-        gates = stack.enter_context(tc.tile_pool(name="gates", bufs=3))
+        quant = stack.enter_context(tc.tile_pool(name="quant", bufs=LEAD + 2))
+        gates = stack.enter_context(tc.tile_pool(name="gates", bufs=4))
         results = stack.enter_context(tc.tile_pool(name="results", bufs=OUT_BUFS))
         psum_t = stack.enter_context(tc.psum_pool(name="psum_t", bufs=2))
         psum_mx = stack.enter_context(tc.psum_pool(name="psum_mx", bufs=6))
@@ -123,87 +123,84 @@ def tile_lstmmirrored_pb_t_kernel(
         codes_of = {}
         planes_of = {}
         gates_of = {}
+        results_of = {}
 
-        def transpose_and_regroup(rnd):
-            grouped = quant.tile([P, ROUND_TILES, SOURCES * P * PACK], BF16, align_bytes=64)
-            grouped_of[rnd] = grouped
-            for j in range(ROUND_TILES):
-                t = rnd * ROUND_TILES + j
-                xt = psum_t.tile([P, 2, SOURCES, P], F32)
-                for source, chunks in enumerate((x_chunks, hist_chunks)):
-                    words = chunks[t // CHUNK_TILES][:, t % CHUNK_TILES, :].bitcast(F32)
-                    for u in range(2):
-                        nc.tensor.transpose(xt[:, u, source, :], words[:, u : D // 2 : 2], identity[:])
-                nc.scalar.copy(
-                    out=grouped[:, j, :].bitcast(F32).rearrange("p (c u) -> p c u", u=2),
-                    in_=xt[:].rearrange("p u s r -> p (s r) u"),
-                )
-
-        def quantise(rnd):
-            codes = quant.tile([P, ROUND_TILES * SOURCES * P], U32, align_bytes=64)
-            planes = quant.tile([P, ROUND_TILES * SOURCES * P], U8, align_bytes=64)
-            codes_of[rnd] = codes
-            planes_of[rnd] = planes
-            nc.vector.quantize_mx(
-                out=codes[:].bitcast(FP8X4),
-                scales=planes[:],
-                in_=grouped_of[rnd][:].rearrange("p j c -> p (j c)"),
+        def transpose_and_regroup(t):
+            grouped = quant.tile([P, SOURCES * P * PACK], BF16, align_bytes=64)
+            grouped_of[t] = grouped
+            xt = psum_t.tile([P, 2, SOURCES, P], F32)
+            for source, chunks in enumerate((x_chunks, hist_chunks)):
+                words = chunks[t // CHUNK_TILES][:, t % CHUNK_TILES, :].bitcast(F32)
+                for u in range(2):
+                    nc.tensor.transpose(xt[:, u, source, :], words[:, u : D // 2 : 2], identity[:])
+            nc.scalar.copy(
+                out=grouped[:].bitcast(F32).rearrange("p (c u) -> p c u", u=2),
+                in_=xt[:].rearrange("p u s r -> p (s r) u"),
             )
 
-        def gate_sums(rnd):
-            pre = gates.tile([P, ROUND_TILES, GATES, D], F32)
-            gates_of[rnd] = pre
-            for j in range(ROUND_TILES):
-                for gate in range(GATES):
-                    acc = psum_mx.tile([P, D], F32)
-                    for source in range(SOURCES):
-                        rows = slice((j * SOURCES + source) * P, (j * SOURCES + source + 1) * P)
-                        w = gate * SOURCES + source
-                        nc.tensor.matmul_mx(
-                            out=acc[:],
-                            lhsT=codes_of[rnd][:, rows].bitcast(FP8X4),
-                            lhsT_scale=planes_of[rnd][:, rows],
-                            rhs=w_words[:, w, :].bitcast(FP8X4),
-                            rhs_scale=w_planes[:, w, :],
-                            start=(source == 0),
-                            stop=(source == SOURCES - 1),
-                        )
-                    nc.vector.tensor_tensor(out=pre[:, j, gate, :], in0=acc[:], in1=bias[:, gate, :], op=ADD)
+        def quantise(t):
+            codes = quant.tile([P, SOURCES * P], U32, align_bytes=64)
+            planes = quant.tile([P, SOURCES * P], U8, align_bytes=64)
+            codes_of[t] = codes
+            planes_of[t] = planes
+            nc.vector.quantize_mx(out=codes[:].bitcast(FP8X4), scales=planes[:], in_=grouped_of[t][:])
 
-        def sigmoids(rnd):
-            for j in range(ROUND_TILES):
-                both = gates_of[rnd][:, j, :, :].rearrange("p g d -> p (g d)")
-                nc.scalar.activation(out=both, in_=both, func=SIGMOID)
+        def gate_sums(t):
+            pre = gates.tile([P, GATES, D], F32)
+            gates_of[t] = pre
+            for gate in range(GATES):
+                acc = psum_mx.tile([P, D], F32)
+                for source in range(SOURCES):
+                    rows = slice(source * P, (source + 1) * P)
+                    w = gate * SOURCES + source
+                    nc.tensor.matmul_mx(
+                        out=acc[:],
+                        lhsT=codes_of[t][:, rows].bitcast(FP8X4),
+                        lhsT_scale=planes_of[t][:, rows],
+                        rhs=w_words[:, w, :].bitcast(FP8X4),
+                        rhs_scale=w_planes[:, w, :],
+                        start=(source == 0),
+                        stop=(source == SOURCES - 1),
+                    )
+                nc.vector.tensor_tensor(out=pre[:, gate, :], in0=acc[:], in1=bias[:, gate, :], op=ADD)
 
-        def cell_and_hidden(rnd):
-            t = rnd * ROUND_TILES
-            tiles = slice(t, t + ROUND_TILES)
-            in_chunk = slice(t % CHUNK_TILES, t % CHUNK_TILES + ROUND_TILES)
-            c_out = results.tile([P, ROUND_TILES, D], F32)
-            h_out = results.tile([P, ROUND_TILES, D], F32)
+        def sigmoids(t):
+            both = gates_of[t][:].rearrange("p g d -> p (g d)")
+            nc.scalar.activation(out=both, in_=both, func=SIGMOID)
+
+        def cell_and_hidden(t):
+            j = t % STORE_TILES
+            if j == 0:
+                c_out = results.tile([P, STORE_TILES, D], F32)
+                h_out = results.tile([P, STORE_TILES, D], F32)
+                results_of[t // STORE_TILES] = (c_out, h_out)
+            c_out, h_out = results_of[t // STORE_TILES]
             nc.vector.scalar_tensor_tensor(
-                out=c_out[:],
-                in0=gates_of[rnd][:, :, 0, :],
+                out=c_out[:, j, :],
+                in0=gates_of[t][:, 0, :],
                 scalar=gain[:],
-                in1=ig_chunks[t // CHUNK_TILES][:, in_chunk, :],
+                in1=ig_chunks[t // CHUNK_TILES][:, t % CHUNK_TILES, :],
                 op0=MULT,
                 op1=ADD,
             )
-            nc.sync.dma_start(out=c_rows[:, tiles, :], in_=c_out[:])
-            nc.vector.tensor_tensor(out=h_out[:], in0=gates_of[rnd][:, :, 1, :], in1=c_out[:], op=MULT)
-            nc.sync.dma_start(out=h_rows[:, tiles, :], in_=h_out[:])
+            nc.gpsimd.tensor_tensor(out=h_out[:, j, :], in0=gates_of[t][:, 1, :], in1=c_out[:, j, :], op=MULT)
+            if j == STORE_TILES - 1:
+                tiles = slice(t + 1 - STORE_TILES, t + 1)
+                nc.sync.dma_start(out=c_rows[:, tiles, :], in_=c_out[:])
+                nc.sync.dma_start(out=h_rows[:, tiles, :], in_=h_out[:])
 
-        transpose_and_regroup(0)
-        quantise(0)
+        for t in range(LEAD):
+            transpose_and_regroup(t)
+            quantise(t)
         nc.vector.tensor_copy(out=gain[:], in_=gain_bf[:])
-        for step in range(ROUNDS + 1):
-            if step + 1 < ROUNDS:
-                transpose_and_regroup(step + 1)
-            if step < ROUNDS:
+        for step in range(ROW_TILES + 1):
+            if step + LEAD < ROW_TILES:
+                transpose_and_regroup(step + LEAD)
+            if step < ROW_TILES:
                 gate_sums(step)
-            if step + 1 < ROUNDS:
-                quantise(step + 1)
-            if step < ROUNDS:
+            if step + LEAD < ROW_TILES:
+                quantise(step + LEAD)
+            if step < ROW_TILES:
                 sigmoids(step)
             if step >= 1:
                 cell_and_hidden(step - 1)

@@ -66,7 +66,8 @@ def tile_lstmmirrored_pb_t_kernel(
         gates = stack.enter_context(tc.tile_pool(name="gates", bufs=4))
         results = stack.enter_context(tc.tile_pool(name="results", bufs=OUT_BUFS))
         psum_t = stack.enter_context(tc.psum_pool(name="psum_t", bufs=2))
-        psum_mx = stack.enter_context(tc.psum_pool(name="psum_mx", bufs=6))
+        psum_ig = stack.enter_context(tc.psum_pool(name="psum_ig", bufs=2))
+        psum_mx = stack.enter_context(tc.psum_pool(name="psum_mx", bufs=4))
         stack.enter_context(tc.manual_schedule())
 
         w_words = const.tile([P, GATES * SOURCES, D], U32, align_bytes=64)
@@ -76,10 +77,12 @@ def tile_lstmmirrored_pb_t_kernel(
         gain = const.tile([P, 1], F32)
         table_warm = const.tile([P, 1], F32)
         identity = const.tile([P, P], F32)
+        identity_bf = const.tile([P, P], BF16)
 
         nc.vector.memset(w_planes[:].rearrange("p w n -> p (w n)").bitcast(I32), 0)
         nc.vector.memset(table_warm[:], 0.0)
         make_identity(nc, identity[:])
+        make_identity(nc, identity_bf[:])
 
         x_chunks = []
         hist_chunks = []
@@ -124,6 +127,7 @@ def tile_lstmmirrored_pb_t_kernel(
         planes_of = {}
         gates_of = {}
         results_of = {}
+        ig_of = {}
 
         def transpose_and_regroup(t):
             grouped = quant.tile([P, SOURCES * P * PACK], BF16, align_bytes=64)
@@ -146,6 +150,15 @@ def tile_lstmmirrored_pb_t_kernel(
             nc.vector.quantize_mx(out=codes[:].bitcast(FP8X4), scales=planes[:], in_=grouped_of[t][:])
 
         def gate_sums(t):
+            ig_ps = psum_ig.tile([P, D], F32)
+            ig_of[t] = ig_ps
+            nc.tensor.matmul(
+                out=ig_ps[:],
+                lhsT=identity_bf[:],
+                rhs=ig_chunks[t // CHUNK_TILES][:, t % CHUNK_TILES, :],
+                start=True,
+                stop=True,
+            )
             pre = gates.tile([P, GATES, D], F32)
             gates_of[t] = pre
             for gate in range(GATES):
@@ -179,7 +192,7 @@ def tile_lstmmirrored_pb_t_kernel(
                 out=c_out[:, j, :],
                 in0=gates_of[t][:, 0, :],
                 scalar=gain[:],
-                in1=ig_chunks[t // CHUNK_TILES][:, t % CHUNK_TILES, :],
+                in1=ig_of[t][:],
                 op0=MULT,
                 op1=ADD,
             )
@@ -198,9 +211,8 @@ def tile_lstmmirrored_pb_t_kernel(
                 transpose_and_regroup(step + LEAD)
             if step < ROW_TILES:
                 gate_sums(step)
-            if step + LEAD < ROW_TILES:
-                quantise(step + LEAD)
-            if step < ROW_TILES:
                 sigmoids(step)
             if step >= 1:
                 cell_and_hidden(step - 1)
+            if step + LEAD < ROW_TILES:
+                quantise(step + LEAD)

@@ -150,15 +150,6 @@ def tile_lstmmirrored_pb_t_kernel(
             nc.vector.quantize_mx(out=codes[:].bitcast(FP8X4), scales=planes[:], in_=grouped_of[t][:])
 
         def gate_sums(t):
-            ig_ps = psum_ig.tile([P, D], F32)
-            ig_of[t] = ig_ps
-            nc.tensor.matmul(
-                out=ig_ps[:],
-                lhsT=identity_bf[:],
-                rhs=ig_chunks[t // CHUNK_TILES][:, t % CHUNK_TILES, :],
-                start=True,
-                stop=True,
-            )
             pre = gates.tile([P, GATES, D], F32)
             gates_of[t] = pre
             for gate in range(GATES):
@@ -176,6 +167,17 @@ def tile_lstmmirrored_pb_t_kernel(
                         stop=(source == SOURCES - 1),
                     )
                 nc.vector.tensor_tensor(out=pre[:, gate, :], in0=acc[:], in1=bias[:, gate, :], op=ADD)
+
+        def ig_to_psum(t):
+            ig_ps = psum_ig.tile([P, D], F32)
+            ig_of[t] = ig_ps
+            nc.tensor.matmul(
+                out=ig_ps[:],
+                lhsT=identity_bf[:],
+                rhs=ig_chunks[t // CHUNK_TILES][:, t % CHUNK_TILES, :],
+                start=True,
+                stop=True,
+            )
 
         def sigmoids(t):
             both = gates_of[t][:].rearrange("p g d -> p (g d)")
@@ -211,6 +213,7 @@ def tile_lstmmirrored_pb_t_kernel(
                 transpose_and_regroup(step + LEAD)
             if step < ROW_TILES:
                 gate_sums(step)
+                ig_to_psum(step)
                 sigmoids(step)
             if step >= 1:
                 cell_and_hidden(step - 1)

@@ -20,8 +20,7 @@ PACK = 4
 ROW_TILES = BATCH // P
 STORE_TILES = 2
 LEAD = 2
-CHUNK_TILES = 4
-CHUNKS = ROW_TILES // CHUNK_TILES
+MAX_CHUNK_TILES = 8
 GATES = 2
 SOURCES = 2
 OUT_BUFS = 8
@@ -82,28 +81,34 @@ def tile_lstmmirrored_pb_t_kernel(
         nc.vector.memset(w_planes[:].rearrange("p w n -> p (w n)").bitcast(I32), 0)
         nc.vector.memset(table_warm[:], 0.0)
         make_identity(nc, identity[:])
-        make_identity(nc, identity_bf[:])
 
-        x_chunks = []
-        hist_chunks = []
-        ig_chunks = []
-        for chunk in range(CHUNKS):
-            x_chunk = inputs.tile([P, CHUNK_TILES, D], BF16, name="x%d" % chunk)
-            hist_chunk = inputs.tile([P, CHUNK_TILES, D], BF16, name="hist%d" % chunk)
-            ig_chunk = inputs.tile([P, CHUNK_TILES, D], BF16, name="ig%d" % chunk)
-            x_chunks.append(x_chunk)
-            hist_chunks.append(hist_chunk)
-            ig_chunks.append(ig_chunk)
+        chunks = []
+        first = 0
+        count = LEAD
+        while first < ROW_TILES:
+            chunks.append((first, count))
+            first += count
+            count = min(first, MAX_CHUNK_TILES)
 
-        def chunk_rows(chunk):
-            return slice(chunk * CHUNK_TILES, (chunk + 1) * CHUNK_TILES)
+        x_of = {}
+        hist_of = {}
+        ig_of = {}
 
-        nc.scalar.dma_start(out=x_chunks[0][:], in_=x_rows[:, chunk_rows(0), :])
-        nc.scalar.dma_start(out=hist_chunks[0][:], in_=hist_rows[:, chunk_rows(0), :])
-        nc.scalar.dma_start(out=gain_bf[:], in_=carousel.partition_broadcast(P))
-        nc.scalar.dma_start(out=bias[:, 0, :], in_=b_f.partition_broadcast(P))
-        nc.scalar.dma_start(out=bias[:, 1, :], in_=b_o.partition_broadcast(P))
+        def load(queue, rows, tile_of, name, first, count):
+            chunk = inputs.tile([P, count, D], BF16, name="%s%d" % (name, first))
+            queue.dma_start(out=chunk[:], in_=rows[:, first : first + count, :])
+            for j in range(count):
+                tile_of[first + j] = chunk[:, j, :]
+
+        for first, count in chunks[:2]:
+            load(nc.scalar, x_rows, x_of, "x", first, count)
+            load(nc.scalar, hist_rows, hist_of, "hist", first, count)
         nc.scalar.activation(out=table_warm[:], in_=table_warm[:], func=SIGMOID)
+        nc.gpsimd.dma_start(out=bias[:, 0, :], in_=b_f.partition_broadcast(P))
+        nc.gpsimd.dma_start(out=bias[:, 1, :], in_=b_o.partition_broadcast(P))
+        nc.gpsimd.dma_start(out=gain_bf[:], in_=carousel.partition_broadcast(P))
+        make_identity(nc, identity_bf[:])
+        nc.gpsimd.tensor_copy(out=gain[:], in_=gain_bf[:])
 
         for w in range(GATES * SOURCES):
             for r in range(4):
@@ -116,25 +121,26 @@ def tile_lstmmirrored_pb_t_kernel(
                 out=w_words[:, w, :].bitcast(I32),
                 in_=weight_words[w][0].rearrange("p n t -> p (n t)").bitcast(I32),
             )
-        nc.sync.dma_start(out=ig_chunks[0][:], in_=ig_rows[:, chunk_rows(0), :])
-        for chunk in range(1, CHUNKS):
-            nc.sync.dma_start(out=x_chunks[chunk][:], in_=x_rows[:, chunk_rows(chunk), :])
-            nc.sync.dma_start(out=hist_chunks[chunk][:], in_=hist_rows[:, chunk_rows(chunk), :])
-            nc.sync.dma_start(out=ig_chunks[chunk][:], in_=ig_rows[:, chunk_rows(chunk), :])
+        for first, count in chunks[:2]:
+            load(nc.sync, ig_rows, ig_of, "ig", first, count)
+        for first, count in chunks[2:]:
+            load(nc.sync, x_rows, x_of, "x", first, count)
+            load(nc.sync, hist_rows, hist_of, "hist", first, count)
+            load(nc.sync, ig_rows, ig_of, "ig", first, count)
 
         grouped_of = {}
         codes_of = {}
         planes_of = {}
         gates_of = {}
         results_of = {}
-        ig_of = {}
+        ig_psum_of = {}
 
         def transpose_and_regroup(t):
             grouped = quant.tile([P, SOURCES * P * PACK], BF16, align_bytes=64)
             grouped_of[t] = grouped
             xt = psum_t.tile([P, 2, SOURCES, P], F32)
-            for source, chunks in enumerate((x_chunks, hist_chunks)):
-                words = chunks[t // CHUNK_TILES][:, t % CHUNK_TILES, :].bitcast(F32)
+            for source, tile_of in enumerate((x_of, hist_of)):
+                words = tile_of[t].bitcast(F32)
                 for u in range(2):
                     nc.tensor.transpose(xt[:, u, source, :], words[:, u : D // 2 : 2], identity[:])
             nc.scalar.copy(
@@ -170,18 +176,23 @@ def tile_lstmmirrored_pb_t_kernel(
 
         def ig_to_psum(t):
             ig_ps = psum_ig.tile([P, D], F32)
-            ig_of[t] = ig_ps
+            ig_psum_of[t] = ig_ps
             nc.tensor.matmul(
                 out=ig_ps[:],
                 lhsT=identity_bf[:],
-                rhs=ig_chunks[t // CHUNK_TILES][:, t % CHUNK_TILES, :],
+                rhs=ig_of[t],
                 start=True,
                 stop=True,
             )
 
         def sigmoids(t):
-            both = gates_of[t][:].rearrange("p g d -> p (g d)")
-            nc.scalar.activation(out=both, in_=both, func=SIGMOID)
+            if t < ROW_TILES - 1:
+                both = gates_of[t][:].rearrange("p g d -> p (g d)")
+                nc.scalar.activation(out=both, in_=both, func=SIGMOID)
+            else:
+                for gate in range(GATES):
+                    one = gates_of[t][:, gate, :]
+                    nc.scalar.activation(out=one, in_=one, func=SIGMOID)
 
         def cell_and_hidden(t):
             j = t % STORE_TILES
@@ -194,11 +205,12 @@ def tile_lstmmirrored_pb_t_kernel(
                 out=c_out[:, j, :],
                 in0=gates_of[t][:, 0, :],
                 scalar=gain[:],
-                in1=ig_of[t][:],
+                in1=ig_psum_of[t][:],
                 op0=MULT,
                 op1=ADD,
             )
-            nc.gpsimd.tensor_tensor(out=h_out[:, j, :], in0=gates_of[t][:, 1, :], in1=c_out[:, j, :], op=MULT)
+            multiplier = nc.gpsimd if t < ROW_TILES - 1 else nc.vector
+            multiplier.tensor_tensor(out=h_out[:, j, :], in0=gates_of[t][:, 1, :], in1=c_out[:, j, :], op=MULT)
             if j == STORE_TILES - 1:
                 tiles = slice(t + 1 - STORE_TILES, t + 1)
                 nc.sync.dma_start(out=c_rows[:, tiles, :], in_=c_out[:])
@@ -207,7 +219,6 @@ def tile_lstmmirrored_pb_t_kernel(
         for t in range(LEAD):
             transpose_and_regroup(t)
             quantise(t)
-        nc.vector.tensor_copy(out=gain[:], in_=gain_bf[:])
         for step in range(ROW_TILES + 1):
             if step + LEAD < ROW_TILES:
                 transpose_and_regroup(step + LEAD)

@@ -226,7 +226,7 @@ def tile_lstmmirrored_pb_t_kernel(
                 gate_sums(step)
                 ig_to_psum(step)
                 sigmoids(step)
-            if step >= 1:
-                cell_and_hidden(step - 1)
             if step + LEAD < ROW_TILES:
                 quantise(step + LEAD)
+            if step >= 1:
+                cell_and_hidden(step - 1)

@@ -18,14 +18,17 @@ BATCH = 4096
 D = 512
 PACK = 4
 ROW_TILES = BATCH // P
-STORE_TILES = 2
-LEAD = 2
+PAIR = 2
+PAIRS = ROW_TILES // PAIR
+PAIR_ROWS = PAIR * P
+CHANNEL_TILES = D // P
 MAX_CHUNK_TILES = 8
-GATES = 2
 SOURCES = 2
+FORGET = 0
+OUTPUT = 1
 OUT_BUFS = 8
 
-FLOPS = 2 * BATCH * D * D * GATES * SOURCES
+FLOPS = 2 * BATCH * D * D * 2 * SOURCES
 
 
 def tile_lstmmirrored_pb_t_kernel(
@@ -61,22 +64,21 @@ def tile_lstmmirrored_pb_t_kernel(
     with ExitStack() as stack:
         const = stack.enter_context(tc.tile_pool(name="const", bufs=1))
         inputs = stack.enter_context(tc.tile_pool(name="inputs", bufs=1))
-        quant = stack.enter_context(tc.tile_pool(name="quant", bufs=LEAD + 2))
-        gates = stack.enter_context(tc.tile_pool(name="gates", bufs=4))
+        quant = stack.enter_context(tc.tile_pool(name="quant", bufs=2))
+        gates = stack.enter_context(tc.tile_pool(name="gates", bufs=3))
         results = stack.enter_context(tc.tile_pool(name="results", bufs=OUT_BUFS))
-        psum_t = stack.enter_context(tc.psum_pool(name="psum_t", bufs=2))
-        psum_ig = stack.enter_context(tc.psum_pool(name="psum_ig", bufs=2))
-        psum_mx = stack.enter_context(tc.psum_pool(name="psum_mx", bufs=4))
+        psum = stack.enter_context(tc.psum_pool(name="psum", bufs=2))
         stack.enter_context(tc.manual_schedule())
 
-        w_words = const.tile([P, GATES * SOURCES, D], U32, align_bytes=64)
-        w_planes = const.tile([P, GATES * SOURCES, D], U8, align_bytes=64)
-        bias = const.tile([P, GATES, D], BF16)
+        w_words = const.tile([P, 2 * SOURCES, D], U32, align_bytes=64)
+        w_planes = const.tile([P, 2 * SOURCES, D], U8, align_bytes=64)
+        bias_o = const.tile([P, D], BF16)
+        bias_f_bf = const.tile([P, CHANNEL_TILES, 2], BF16)
+        bias_f = const.tile([P, CHANNEL_TILES], F32)
         gain_bf = const.tile([P, 1], BF16)
         gain = const.tile([P, 1], F32)
         table_warm = const.tile([P, 1], F32)
         identity = const.tile([P, P], F32)
-        identity_bf = const.tile([P, P], BF16)
 
         nc.vector.memset(w_planes[:].rearrange("p w n -> p (w n)").bitcast(I32), 0)
         nc.vector.memset(table_warm[:], 0.0)
@@ -84,7 +86,7 @@ def tile_lstmmirrored_pb_t_kernel(
 
         chunks = []
         first = 0
-        count = LEAD
+        count = PAIR
         while first < ROW_TILES:
             chunks.append((first, count))
             first += count
@@ -104,19 +106,22 @@ def tile_lstmmirrored_pb_t_kernel(
             load(nc.scalar, x_rows, x_of, "x", first, count)
             load(nc.scalar, hist_rows, hist_of, "hist", first, count)
         nc.scalar.activation(out=table_warm[:], in_=table_warm[:], func=SIGMOID)
-        nc.gpsimd.dma_start(out=bias[:, 0, :], in_=b_f.partition_broadcast(P))
-        nc.gpsimd.dma_start(out=bias[:, 1, :], in_=b_o.partition_broadcast(P))
+        nc.gpsimd.dma_start(
+            out=bias_f_bf[:, :, 0:1],
+            in_=b_f.rearrange("(m p e) -> p m e", p=P, e=1),
+        )
+        nc.gpsimd.dma_start(out=bias_o[:], in_=b_o.partition_broadcast(P))
         nc.gpsimd.dma_start(out=gain_bf[:], in_=carousel.partition_broadcast(P))
-        make_identity(nc, identity_bf[:])
+        nc.gpsimd.tensor_copy(out=bias_f[:], in_=bias_f_bf[:, :, 0])
         nc.gpsimd.tensor_copy(out=gain[:], in_=gain_bf[:])
 
-        for w in range(GATES * SOURCES):
+        for w in range(2 * SOURCES):
             for r in range(4):
                 nc.sync.dma_start(
                     out=w_planes[r:P:32, w, :].bitcast(I32),
                     in_=weight_scales[w][0, r:16:4, :].bitcast(I32),
                 )
-        for w in range(GATES * SOURCES):
+        for w in range(2 * SOURCES):
             nc.sync.dma_start(
                 out=w_words[:, w, :].bitcast(I32),
                 in_=weight_words[w][0].rearrange("p n t -> p (n t)").bitcast(I32),
@@ -131,102 +136,141 @@ def tile_lstmmirrored_pb_t_kernel(
         grouped_of = {}
         codes_of = {}
         planes_of = {}
-        gates_of = {}
+        forget_t_of = {}
+        forget_of = {}
+        output_of = {}
         results_of = {}
-        ig_psum_of = {}
 
-        def transpose_and_regroup(t):
-            grouped = quant.tile([P, SOURCES * P * PACK], BF16, align_bytes=64)
-            grouped_of[t] = grouped
-            xt = psum_t.tile([P, 2, SOURCES, P], F32)
+        def transpose_and_regroup(j):
+            grouped = quant.tile([P, SOURCES, PAIR_ROWS * PACK], BF16, align_bytes=64)
+            grouped_of[j] = grouped
             for source, tile_of in enumerate((x_of, hist_of)):
-                words = tile_of[t].bitcast(F32)
-                for u in range(2):
-                    nc.tensor.transpose(xt[:, u, source, :], words[:, u : D // 2 : 2], identity[:])
-            nc.scalar.copy(
-                out=grouped[:].bitcast(F32).rearrange("p (c u) -> p c u", u=2),
-                in_=xt[:].rearrange("p u s r -> p (s r) u"),
+                xt = psum.tile([P, 2, PAIR_ROWS], F32)
+                for a in range(PAIR):
+                    words = tile_of[PAIR * j + a].bitcast(F32)
+                    for u in range(2):
+                        nc.tensor.transpose(xt[:, u, a * P : (a + 1) * P], words[:, u : D // 2 : 2], identity[:])
+                nc.scalar.copy(
+                    out=grouped[:, source, :].bitcast(F32).rearrange("p (r u) -> p r u", u=2),
+                    in_=xt[:].rearrange("p u r -> p r u"),
+                )
+
+        def quantise(j):
+            codes = quant.tile([P, SOURCES * PAIR_ROWS], U32, align_bytes=64)
+            planes = quant.tile([P, SOURCES * PAIR_ROWS], U8, align_bytes=64)
+            codes_of[j] = codes
+            planes_of[j] = planes
+            nc.vector.quantize_mx(
+                out=codes[:].bitcast(FP8X4),
+                scales=planes[:],
+                in_=grouped_of[j][:].rearrange("p s c -> p (s c)"),
             )
 
-        def quantise(t):
-            codes = quant.tile([P, SOURCES * P], U32, align_bytes=64)
-            planes = quant.tile([P, SOURCES * P], U8, align_bytes=64)
-            codes_of[t] = codes
-            planes_of[t] = planes
-            nc.vector.quantize_mx(out=codes[:].bitcast(FP8X4), scales=planes[:], in_=grouped_of[t][:])
+        def forget_sums(j):
+            banks = []
+            for half in range(CHANNEL_TILES // 2):
+                acc_t = psum.tile([P, 2, PAIR_ROWS], F32)
+                banks.append(acc_t)
+                for i in range(2):
+                    m = 2 * half + i
+                    channels = slice(m * P, (m + 1) * P)
+                    for source in range(SOURCES):
+                        rows = slice(source * PAIR_ROWS, (source + 1) * PAIR_ROWS)
+                        w = FORGET * SOURCES + source
+                        nc.tensor.matmul_mx(
+                            out=acc_t[:, i, :],
+                            lhsT=w_words[:, w, channels].bitcast(FP8X4),
+                            lhsT_scale=w_planes[:, w, channels],
+                            rhs=codes_of[j][:, rows].bitcast(FP8X4),
+                            rhs_scale=planes_of[j][:, rows],
+                            start=(source == 0),
+                            stop=(source == SOURCES - 1),
+                        )
+            return banks
 
-        def gate_sums(t):
-            pre = gates.tile([P, GATES, D], F32)
-            gates_of[t] = pre
-            for gate in range(GATES):
-                acc = psum_mx.tile([P, D], F32)
+        def forget_sigmoids(j, banks):
+            forget_t = gates.tile([P, CHANNEL_TILES, PAIR_ROWS], F32)
+            forget_t_of[j] = forget_t
+            for m in range(CHANNEL_TILES):
+                nc.scalar.activation(
+                    out=forget_t[:, m, :],
+                    in_=banks[m // 2][:, m % 2, :],
+                    func=SIGMOID,
+                    bias=bias_f[:, m : m + 1],
+                )
+
+        def forget_back(j):
+            for a in range(PAIR):
+                forget = psum.tile([P, D], F32)
+                forget_of[PAIR * j + a] = forget
+                for m in range(CHANNEL_TILES):
+                    nc.tensor.transpose(
+                        forget[:, m * P : (m + 1) * P],
+                        forget_t_of[j][:, m, a * P : (a + 1) * P],
+                        identity[:],
+                    )
+
+        def output_sums(j):
+            accs = []
+            for a in range(PAIR):
+                acc = psum.tile([P, D], F32)
+                accs.append(acc)
                 for source in range(SOURCES):
-                    rows = slice(source * P, (source + 1) * P)
-                    w = gate * SOURCES + source
+                    rows = slice(source * PAIR_ROWS + a * P, source * PAIR_ROWS + (a + 1) * P)
+                    w = OUTPUT * SOURCES + source
                     nc.tensor.matmul_mx(
                         out=acc[:],
-                        lhsT=codes_of[t][:, rows].bitcast(FP8X4),
-                        lhsT_scale=planes_of[t][:, rows],
+                        lhsT=codes_of[j][:, rows].bitcast(FP8X4),
+                        lhsT_scale=planes_of[j][:, rows],
                         rhs=w_words[:, w, :].bitcast(FP8X4),
                         rhs_scale=w_planes[:, w, :],
                         start=(source == 0),
                         stop=(source == SOURCES - 1),
                     )
-                nc.vector.tensor_tensor(out=pre[:, gate, :], in0=acc[:], in1=bias[:, gate, :], op=ADD)
+            return accs
 
-        def ig_to_psum(t):
-            ig_ps = psum_ig.tile([P, D], F32)
-            ig_psum_of[t] = ig_ps
-            nc.tensor.matmul(
-                out=ig_ps[:],
-                lhsT=identity_bf[:],
-                rhs=ig_of[t],
-                start=True,
-                stop=True,
-            )
+        def output_bias(j, accs):
+            output = gates.tile([P, PAIR, D], F32)
+            output_of[j] = output
+            for a in range(PAIR):
+                nc.vector.tensor_tensor(out=output[:, a, :], in0=accs[a][:], in1=bias_o[:], op=ADD)
 
-        def sigmoids(t):
-            if t < ROW_TILES - 1:
-                both = gates_of[t][:].rearrange("p g d -> p (g d)")
-                nc.scalar.activation(out=both, in_=both, func=SIGMOID)
-            else:
-                for gate in range(GATES):
-                    one = gates_of[t][:, gate, :]
-                    nc.scalar.activation(out=one, in_=one, func=SIGMOID)
+        def output_sigmoid(j):
+            both = output_of[j][:].rearrange("p a d -> p (a d)")
+            nc.scalar.activation(out=both, in_=both, func=SIGMOID)
 
-        def cell_and_hidden(t):
-            j = t % STORE_TILES
-            if j == 0:
-                c_out = results.tile([P, STORE_TILES, D], F32)
-                h_out = results.tile([P, STORE_TILES, D], F32)
-                results_of[t // STORE_TILES] = (c_out, h_out)
-            c_out, h_out = results_of[t // STORE_TILES]
-            nc.vector.scalar_tensor_tensor(
-                out=c_out[:, j, :],
-                in0=gates_of[t][:, 0, :],
-                scalar=gain[:],
-                in1=ig_psum_of[t][:],
-                op0=MULT,
-                op1=ADD,
-            )
-            multiplier = nc.gpsimd if t < ROW_TILES - 1 else nc.vector
-            multiplier.tensor_tensor(out=h_out[:, j, :], in0=gates_of[t][:, 1, :], in1=c_out[:, j, :], op=MULT)
-            if j == STORE_TILES - 1:
-                tiles = slice(t + 1 - STORE_TILES, t + 1)
-                nc.sync.dma_start(out=c_rows[:, tiles, :], in_=c_out[:])
-                nc.sync.dma_start(out=h_rows[:, tiles, :], in_=h_out[:])
+        def cell_and_hidden(j):
+            c_out = results.tile([P, PAIR, D], F32)
+            h_out = results.tile([P, PAIR, D], F32)
+            for a in range(PAIR):
+                nc.vector.scalar_tensor_tensor(
+                    out=c_out[:, a, :],
+                    in0=forget_of[PAIR * j + a][:],
+                    scalar=gain[:],
+                    in1=ig_of[PAIR * j + a],
+                    op0=MULT,
+                    op1=ADD,
+                )
+                nc.gpsimd.tensor_tensor(out=h_out[:, a, :], in0=output_of[j][:, a, :], in1=c_out[:, a, :], op=MULT)
+            tiles = slice(PAIR * j, PAIR * (j + 1))
+            nc.sync.dma_start(out=c_rows[:, tiles, :], in_=c_out[:])
+            nc.sync.dma_start(out=h_rows[:, tiles, :], in_=h_out[:])
 
-        for t in range(LEAD):
-            transpose_and_regroup(t)
-            quantise(t)
-        for step in range(ROW_TILES + 1):
-            if step + LEAD < ROW_TILES:
-                transpose_and_regroup(step + LEAD)
-            if step < ROW_TILES:
-                gate_sums(step)
-                ig_to_psum(step)
-                sigmoids(step)
-            if step + LEAD < ROW_TILES:
-                quantise(step + LEAD)
-            if step >= 1:
-                cell_and_hidden(step - 1)
+        transpose_and_regroup(0)
+        quantise(0)
+        for j in range(PAIRS + 1):
+            if j + 1 < PAIRS:
+                transpose_and_regroup(j + 1)
+            if j >= 1:
+                forget_back(j - 1)
+                output_sigmoid(j - 1)
+            if j < PAIRS:
+                banks = forget_sums(j)
+                forget_sigmoids(j, banks)
+                accs = output_sums(j)
+            if j >= 1:
+                cell_and_hidden(j - 1)
+            if j + 1 < PAIRS:
+                quantise(j + 1)
+            if j < PAIRS:
+                output_bias(j, accs)

@@ -26,6 +26,8 @@ MAX_CHUNK_TILES = 8
 SOURCES = 2
 FORGET = 0
 OUTPUT = 1
+LEAD = 3
+IG_LAG = 2
 OUT_BUFS = 8
 
 FLOPS = 2 * BATCH * D * D * 2 * SOURCES
@@ -64,7 +66,8 @@ def tile_lstmmirrored_pb_t_kernel(
     with ExitStack() as stack:
         const = stack.enter_context(tc.tile_pool(name="const", bufs=1))
         inputs = stack.enter_context(tc.tile_pool(name="inputs", bufs=1))
-        quant = stack.enter_context(tc.tile_pool(name="quant", bufs=2))
+        staging = stack.enter_context(tc.tile_pool(name="staging", bufs=2))
+        quant = stack.enter_context(tc.tile_pool(name="quant", bufs=LEAD + 2))
         gates = stack.enter_context(tc.tile_pool(name="gates", bufs=3))
         results = stack.enter_context(tc.tile_pool(name="results", bufs=OUT_BUFS))
         psum = stack.enter_context(tc.psum_pool(name="psum", bufs=2))
@@ -84,13 +87,7 @@ def tile_lstmmirrored_pb_t_kernel(
         nc.vector.memset(table_warm[:], 0.0)
         make_identity(nc, identity[:])
 
-        chunks = []
-        first = 0
-        count = PAIR
-        while first < ROW_TILES:
-            chunks.append((first, count))
-            first += count
-            count = min(first, MAX_CHUNK_TILES)
+        chunks = [(0, 2), (2, 2), (4, 4), (8, 4), (12, 4), (16, 8), (24, 8)]
 
         x_of = {}
         hist_of = {}
@@ -106,6 +103,9 @@ def tile_lstmmirrored_pb_t_kernel(
             load(nc.scalar, x_rows, x_of, "x", first, count)
             load(nc.scalar, hist_rows, hist_of, "hist", first, count)
         nc.scalar.activation(out=table_warm[:], in_=table_warm[:], func=SIGMOID)
+        first, count = chunks[2]
+        load(nc.gpsimd, x_rows, x_of, "x", first, count)
+        load(nc.gpsimd, hist_rows, hist_of, "hist", first, count)
         nc.gpsimd.dma_start(
             out=bias_f_bf[:, :, 0:1],
             in_=b_f.rearrange("(m p e) -> p m e", p=P, e=1),
@@ -126,13 +126,14 @@ def tile_lstmmirrored_pb_t_kernel(
                 out=w_words[:, w, :].bitcast(I32),
                 in_=weight_words[w][0].rearrange("p n t -> p (n t)").bitcast(I32),
             )
-        for first, count in chunks[:2]:
-            load(nc.sync, ig_rows, ig_of, "ig", first, count)
-        for first, count in chunks[2:]:
-            load(nc.sync, x_rows, x_of, "x", first, count)
-            load(nc.sync, hist_rows, hist_of, "hist", first, count)
-            load(nc.sync, ig_rows, ig_of, "ig", first, count)
+        for i in range(3, len(chunks) + IG_LAG):
+            if i < len(chunks):
+                load(nc.sync, x_rows, x_of, "x", chunks[i][0], chunks[i][1])
+                load(nc.sync, hist_rows, hist_of, "hist", chunks[i][0], chunks[i][1])
+            for k in range(0 if i == 3 else i - IG_LAG, i - IG_LAG + 1):
+                load(nc.sync, ig_rows, ig_of, "ig", chunks[k][0], chunks[k][1])
 
+        turned_of = {}
         grouped_of = {}
         codes_of = {}
         planes_of = {}
@@ -141,19 +142,26 @@ def tile_lstmmirrored_pb_t_kernel(
         output_of = {}
         results_of = {}
 
-        def transpose_and_regroup(j):
-            grouped = quant.tile([P, SOURCES, PAIR_ROWS * PACK], BF16, align_bytes=64)
-            grouped_of[j] = grouped
-            for source, tile_of in enumerate((x_of, hist_of)):
+        def transposes(j):
+            turned_of[j] = []
+            for tile_of in (x_of, hist_of):
                 xt = psum.tile([P, 2, PAIR_ROWS], F32)
+                turned_of[j].append(xt)
                 for a in range(PAIR):
                     words = tile_of[PAIR * j + a].bitcast(F32)
                     for u in range(2):
                         nc.tensor.transpose(xt[:, u, a * P : (a + 1) * P], words[:, u : D // 2 : 2], identity[:])
-                nc.scalar.copy(
-                    out=grouped[:, source, :].bitcast(F32).rearrange("p (r u) -> p r u", u=2),
-                    in_=xt[:].rearrange("p u r -> p r u"),
-                )
+
+        def regroup(j, hist_on_vector):
+            grouped = staging.tile([P, SOURCES, PAIR_ROWS * PACK], BF16, align_bytes=64)
+            grouped_of[j] = grouped
+            for source in range(SOURCES):
+                out = grouped[:, source, :].bitcast(F32).rearrange("p (r u) -> p r u", u=2)
+                in_ = turned_of[j][source][:].rearrange("p u r -> p r u")
+                if source == 1 and hist_on_vector:
+                    nc.vector.tensor_copy(out=out, in_=in_)
+                else:
+                    nc.scalar.copy(out=out, in_=in_)
 
         def quantise(j):
             codes = quant.tile([P, SOURCES * PAIR_ROWS], U32, align_bytes=64)
@@ -236,13 +244,20 @@ def tile_lstmmirrored_pb_t_kernel(
                 nc.vector.tensor_tensor(out=output[:, a, :], in0=accs[a][:], in1=bias_o[:], op=ADD)
 
         def output_sigmoid(j):
-            both = output_of[j][:].rearrange("p a d -> p (a d)")
-            nc.scalar.activation(out=both, in_=both, func=SIGMOID)
+            if j < PAIRS - 1:
+                both = output_of[j][:].rearrange("p a d -> p (a d)")
+                nc.scalar.activation(out=both, in_=both, func=SIGMOID)
+            else:
+                for a in range(PAIR):
+                    one = output_of[j][:, a, :]
+                    nc.scalar.activation(out=one, in_=one, func=SIGMOID)
 
         def cell_and_hidden(j):
             c_out = results.tile([P, PAIR, D], F32)
             h_out = results.tile([P, PAIR, D], F32)
-            for a in range(PAIR):
+            tiles = slice(PAIR * j, PAIR * (j + 1))
+
+            def cell(a):
                 nc.vector.scalar_tensor_tensor(
                     out=c_out[:, a, :],
                     in0=forget_of[PAIR * j + a][:],
@@ -251,26 +266,48 @@ def tile_lstmmirrored_pb_t_kernel(
                     op0=MULT,
                     op1=ADD,
                 )
-                nc.gpsimd.tensor_tensor(out=h_out[:, a, :], in0=output_of[j][:, a, :], in1=c_out[:, a, :], op=MULT)
-            tiles = slice(PAIR * j, PAIR * (j + 1))
-            nc.sync.dma_start(out=c_rows[:, tiles, :], in_=c_out[:])
-            nc.sync.dma_start(out=h_rows[:, tiles, :], in_=h_out[:])
 
-        transpose_and_regroup(0)
-        quantise(0)
+            def hidden(engine, a):
+                engine.tensor_tensor(out=h_out[:, a, :], in0=output_of[j][:, a, :], in1=c_out[:, a, :], op=MULT)
+
+            if j < PAIRS - 1:
+                for a in range(PAIR):
+                    cell(a)
+                    hidden(nc.gpsimd, a)
+                nc.sync.dma_start(out=c_rows[:, tiles, :], in_=c_out[:])
+                nc.sync.dma_start(out=h_rows[:, tiles, :], in_=h_out[:])
+            else:
+                for a in range(PAIR):
+                    cell(a)
+                    nc.sync.dma_start(out=c_rows[:, PAIR * j + a, :], in_=c_out[:, a, :])
+                for a in range(PAIR):
+                    hidden(nc.vector, a)
+                    nc.sync.dma_start(out=h_rows[:, PAIR * j + a, :], in_=h_out[:, a, :])
+
+        for j in range(LEAD):
+            transposes(j)
+            regroup(j, True)
+            quantise(j)
         for j in range(PAIRS + 1):
-            if j + 1 < PAIRS:
-                transpose_and_regroup(j + 1)
+            last = j == PAIRS - 1
+            if j + LEAD < PAIRS:
+                transposes(j + LEAD)
+                regroup(j + LEAD, j == 0)
             if j >= 1:
                 forget_back(j - 1)
                 output_sigmoid(j - 1)
             if j < PAIRS:
-                banks = forget_sums(j)
+                if last:
+                    accs = output_sums(j)
+                    banks = forget_sums(j)
+                else:
+                    banks = forget_sums(j)
                 forget_sigmoids(j, banks)
-                accs = output_sums(j)
+                if not last:
+                    accs = output_sums(j)
             if j >= 1:
                 cell_and_hidden(j - 1)
-            if j + 1 < PAIRS:
-                quantise(j + 1)
+            if j + LEAD < PAIRS:
+                quantise(j + LEAD)
             if j < PAIRS:
                 output_bias(j, accs)

@@ -75,16 +75,23 @@ def tile_lstmmirrored_pb_t_kernel(
 
         w_words = const.tile([P, 2 * SOURCES, D], U32, align_bytes=64)
         w_planes = const.tile([P, 2 * SOURCES, D], U8, align_bytes=64)
-        bias_o = const.tile([P, D], BF16)
-        bias_f_bf = const.tile([P, CHANNEL_TILES, 2], BF16)
+        bias_o_rows = const.tile([P, D], BF16)
+        bias_o = const.tile([P, D], F32)
+        bias_f_rows = const.tile([P, P], BF16)
+        bias_f_rows_f32 = const.tile([P, P], F32)
         bias_f = const.tile([P, CHANNEL_TILES], F32)
-        gain_bf = const.tile([P, 1], BF16)
+        gain_rows = const.tile([P, 2], BF16)
         gain = const.tile([P, 1], F32)
+        ones = const.tile([P, P], BF16)
         table_warm = const.tile([P, 1], F32)
         identity = const.tile([P, P], F32)
 
         nc.vector.memset(w_planes[:].rearrange("p w n -> p (w n)").bitcast(I32), 0)
         nc.vector.memset(table_warm[:], 0.0)
+        nc.vector.memset(bias_f_rows[:], 0.0)
+        nc.vector.memset(bias_o_rows[:], 0.0)
+        nc.vector.memset(gain_rows[:], 0.0)
+        nc.vector.memset(ones[:], 1.0)
         make_identity(nc, identity[:])
 
         chunks = [(0, 2), (2, 2), (4, 4), (8, 4), (12, 4), (16, 8), (24, 8)]
@@ -106,14 +113,9 @@ def tile_lstmmirrored_pb_t_kernel(
         first, count = chunks[2]
         load(nc.gpsimd, x_rows, x_of, "x", first, count)
         load(nc.gpsimd, hist_rows, hist_of, "hist", first, count)
-        nc.gpsimd.dma_start(
-            out=bias_f_bf[:, :, 0:1],
-            in_=b_f.rearrange("(m p e) -> p m e", p=P, e=1),
-        )
-        nc.gpsimd.dma_start(out=bias_o[:], in_=b_o.partition_broadcast(P))
-        nc.gpsimd.dma_start(out=gain_bf[:], in_=carousel.partition_broadcast(P))
-        nc.gpsimd.tensor_copy(out=bias_f[:], in_=bias_f_bf[:, :, 0])
-        nc.gpsimd.tensor_copy(out=gain[:], in_=gain_bf[:])
+        nc.gpsimd.dma_start(out=bias_f_rows[0:CHANNEL_TILES, :], in_=b_f.rearrange("(m p) -> m p", p=P))
+        nc.gpsimd.dma_start(out=bias_o_rows[0:1, :], in_=b_o.rearrange("(e d) -> e d", e=1))
+        nc.gpsimd.dma_start(out=gain_rows[0:1, 0:1], in_=carousel.rearrange("(e d) -> e d", e=1))
 
         for w in range(2 * SOURCES):
             for r in range(4):
@@ -284,10 +286,26 @@ def tile_lstmmirrored_pb_t_kernel(
                     hidden(nc.vector, a)
                     nc.sync.dma_start(out=h_rows[:, PAIR * j + a, :], in_=h_out[:, a, :])
 
+        def spread_bias_f():
+            acc = psum.tile([P, D], F32)
+            nc.tensor.transpose(acc[:, 0:P], bias_f_rows_f32[:], identity[:])
+            nc.vector.tensor_copy(out=bias_f[:], in_=acc[:, 0:CHANNEL_TILES])
+
+        def spread_bias_o_and_gain():
+            forget = psum.tile([P, D], F32)
+            nc.tensor.matmul(out=forget[:], lhsT=ones[:], rhs=bias_o_rows[:], start=True, stop=True)
+            nc.vector.tensor_copy(out=bias_o[:], in_=forget[:])
+            forget = psum.tile([P, D], F32)
+            nc.tensor.matmul(out=forget[:, 0:2], lhsT=ones[:], rhs=gain_rows[:], start=True, stop=True)
+            nc.vector.tensor_copy(out=gain[:], in_=forget[:, 0:1])
+
         for j in range(LEAD):
             transposes(j)
             regroup(j, True)
             quantise(j)
+            if j == 1:
+                nc.vector.tensor_copy(out=bias_f_rows_f32[:], in_=bias_f_rows[:])
+        spread_bias_f()
         for j in range(PAIRS + 1):
             last = j == PAIRS - 1
             if j + LEAD < PAIRS:
@@ -305,6 +323,8 @@ def tile_lstmmirrored_pb_t_kernel(
                 forget_sigmoids(j, banks)
                 if not last:
                     accs = output_sums(j)
+            if j == 0:
+                spread_bias_o_and_gain()
             if j >= 1:
                 cell_and_hidden(j - 1)
             if j + LEAD < PAIRS:

@@ -83,15 +83,17 @@ def tile_lstmmirrored_pb_t_kernel(
         gain_rows = const.tile([P, 2], BF16)
         gain = const.tile([P, 1], F32)
         ones = const.tile([P, P], BF16)
+        zeros = const.tile([P, D], BF16)
         table_warm = const.tile([P, 1], F32)
         identity = const.tile([P, P], F32)
 
         nc.vector.memset(w_planes[:].rearrange("p w n -> p (w n)").bitcast(I32), 0)
+        nc.vector.memset(ones[:], 1.0)
+        nc.vector.memset(zeros[:], 0.0)
         nc.vector.memset(table_warm[:], 0.0)
         nc.vector.memset(bias_f_rows[:], 0.0)
         nc.vector.memset(bias_o_rows[:], 0.0)
         nc.vector.memset(gain_rows[:], 0.0)
-        nc.vector.memset(ones[:], 1.0)
         make_identity(nc, identity[:])
 
         chunks = [(0, 2), (2, 2), (4, 4), (8, 4), (12, 4), (16, 8), (24, 8)]
@@ -272,12 +274,19 @@ def tile_lstmmirrored_pb_t_kernel(
             def hidden(engine, a):
                 engine.tensor_tensor(out=h_out[:, a, :], in0=output_of[j][:, a, :], in1=c_out[:, a, :], op=MULT)
 
-            if j < PAIRS - 1:
+            if j < PAIRS - 2:
                 for a in range(PAIR):
                     cell(a)
                     hidden(nc.gpsimd, a)
                 nc.sync.dma_start(out=c_rows[:, tiles, :], in_=c_out[:])
                 nc.sync.dma_start(out=h_rows[:, tiles, :], in_=h_out[:])
+            elif j == PAIRS - 2:
+                for a in range(PAIR):
+                    cell(a)
+                    hidden(nc.gpsimd, a)
+                nc.sync.dma_start(out=c_rows[:, tiles, :], in_=c_out[:])
+                for a in range(PAIR):
+                    nc.sync.dma_start(out=h_rows[:, PAIR * j + a, :], in_=h_out[:, a, :])
             else:
                 for a in range(PAIR):
                     cell(a)
@@ -285,6 +294,11 @@ def tile_lstmmirrored_pb_t_kernel(
                 for a in range(PAIR):
                     hidden(nc.vector, a)
                     nc.sync.dma_start(out=h_rows[:, PAIR * j + a, :], in_=h_out[:, a, :])
+
+        def keep_warm(count):
+            for i in range(count):
+                acc_t = psum.tile([P, 2, PAIR_ROWS], F32)
+                nc.tensor.matmul(out=acc_t[:].rearrange("p i r -> p (i r)"), lhsT=ones[:], rhs=zeros[:], start=True, stop=True)
 
         def spread_bias_f():
             acc = psum.tile([P, D], F32)
@@ -299,8 +313,10 @@ def tile_lstmmirrored_pb_t_kernel(
             nc.tensor.matmul(out=forget[:, 0:2], lhsT=ones[:], rhs=gain_rows[:], start=True, stop=True)
             nc.vector.tensor_copy(out=gain[:], in_=forget[:, 0:1])
 
+        keep_warm(4)
         for j in range(LEAD):
             transposes(j)
+            keep_warm(2)
             regroup(j, True)
             quantise(j)
             if j == 1:
@@ -315,14 +331,9 @@ def tile_lstmmirrored_pb_t_kernel(
                 forget_back(j - 1)
                 output_sigmoid(j - 1)
             if j < PAIRS:
-                if last:
-                    accs = output_sums(j)
-                    banks = forget_sums(j)
-                else:
-                    banks = forget_sums(j)
+                banks = forget_sums(j)
                 forget_sigmoids(j, banks)
-                if not last:
-                    accs = output_sums(j)
+                accs = output_sums(j)
             if j == 0:
                 spread_bias_o_and_gain()
             if j >= 1:

@@ -274,17 +274,17 @@ def tile_lstmmirrored_pb_t_kernel(
             def hidden(engine, a):
                 engine.tensor_tensor(out=h_out[:, a, :], in0=output_of[j][:, a, :], in1=c_out[:, a, :], op=MULT)
 
-            if j < PAIRS - 2:
+            if j < PAIRS - 5:
                 for a in range(PAIR):
                     cell(a)
                     hidden(nc.gpsimd, a)
                 nc.sync.dma_start(out=c_rows[:, tiles, :], in_=c_out[:])
                 nc.sync.dma_start(out=h_rows[:, tiles, :], in_=h_out[:])
-            elif j == PAIRS - 2:
+            elif j < PAIRS - 1:
                 for a in range(PAIR):
                     cell(a)
                     hidden(nc.gpsimd, a)
-                nc.sync.dma_start(out=c_rows[:, tiles, :], in_=c_out[:])
+                    nc.sync.dma_start(out=c_rows[:, PAIR * j + a, :], in_=c_out[:, a, :])
                 for a in range(PAIR):
                     nc.sync.dma_start(out=h_rows[:, PAIR * j + a, :], in_=h_out[:, a, :])
             else:

@@ -80,6 +80,8 @@ def tile_lstmmirrored_pb_t_kernel(
         bias_f_rows = const.tile([P, P], BF16)
         bias_f_rows_f32 = const.tile([P, P], F32)
         bias_f = const.tile([P, CHANNEL_TILES], F32)
+        bias_f_row = const.tile([P, D], BF16)
+        bias_f_all = const.tile([P, D], F32)
         gain_rows = const.tile([P, 2], BF16)
         gain = const.tile([P, 1], F32)
         ones = const.tile([P, P], BF16)
@@ -93,6 +95,7 @@ def tile_lstmmirrored_pb_t_kernel(
         nc.vector.memset(table_warm[:], 0.0)
         nc.vector.memset(bias_f_rows[:], 0.0)
         nc.vector.memset(bias_o_rows[:], 0.0)
+        nc.vector.memset(bias_f_row[:], 0.0)
         nc.vector.memset(gain_rows[:], 0.0)
         make_identity(nc, identity[:])
 
@@ -116,6 +119,7 @@ def tile_lstmmirrored_pb_t_kernel(
         load(nc.gpsimd, x_rows, x_of, "x", first, count)
         load(nc.gpsimd, hist_rows, hist_of, "hist", first, count)
         nc.gpsimd.dma_start(out=bias_f_rows[0:CHANNEL_TILES, :], in_=b_f.rearrange("(m p) -> m p", p=P))
+        nc.gpsimd.dma_start(out=bias_f_row[0:1, :], in_=b_f.rearrange("(e d) -> e d", e=1))
         nc.gpsimd.dma_start(out=bias_o_rows[0:1, :], in_=b_o.rearrange("(e d) -> e d", e=1))
         nc.gpsimd.dma_start(out=gain_rows[0:1, 0:1], in_=carousel.rearrange("(e d) -> e d", e=1))
 
@@ -178,49 +182,51 @@ def tile_lstmmirrored_pb_t_kernel(
                 in_=grouped_of[j][:].rearrange("p s c -> p (s c)"),
             )
 
-        def forget_sums(j):
-            banks = []
-            for half in range(CHANNEL_TILES // 2):
-                acc_t = psum.tile([P, 2, PAIR_ROWS], F32)
-                banks.append(acc_t)
-                for i in range(2):
-                    m = 2 * half + i
-                    channels = slice(m * P, (m + 1) * P)
-                    for source in range(SOURCES):
-                        rows = slice(source * PAIR_ROWS, (source + 1) * PAIR_ROWS)
-                        w = FORGET * SOURCES + source
-                        nc.tensor.matmul_mx(
-                            out=acc_t[:, i, :],
-                            lhsT=w_words[:, w, channels].bitcast(FP8X4),
-                            lhsT_scale=w_planes[:, w, channels],
-                            rhs=codes_of[j][:, rows].bitcast(FP8X4),
-                            rhs_scale=planes_of[j][:, rows],
-                            start=(source == 0),
-                            stop=(source == SOURCES - 1),
-                        )
-            return banks
+        def forget_sums_rows(j):
+            acc_f = psum.tile([P, D], F32, bufs=1)
+            for source in range(SOURCES):
+                rows = slice(source * PAIR_ROWS + P, source * PAIR_ROWS + 2 * P)
+                w = FORGET * SOURCES + source
+                nc.tensor.matmul_mx(
+                    out=acc_f[:],
+                    lhsT=codes_of[j][:, rows].bitcast(FP8X4),
+                    lhsT_scale=planes_of[j][:, rows],
+                    rhs=w_words[:, w, :].bitcast(FP8X4),
+                    rhs_scale=w_planes[:, w, :],
+                    start=(source == 0),
+                    stop=(source == SOURCES - 1),
+                )
+            return acc_f
 
-        def forget_sigmoids(j, banks):
-            forget_t = gates.tile([P, CHANNEL_TILES, PAIR_ROWS], F32)
+        def forget_sums_turned(j):
+            acc_t = psum.tile([P, CHANNEL_TILES, P], F32, bufs=1)
+            for m in range(CHANNEL_TILES):
+                channels = slice(m * P, (m + 1) * P)
+                for source in range(SOURCES):
+                    rows = slice(source * PAIR_ROWS, source * PAIR_ROWS + P)
+                    w = FORGET * SOURCES + source
+                    nc.tensor.matmul_mx(
+                        out=acc_t[:, m, :],
+                        lhsT=w_words[:, w, channels].bitcast(FP8X4),
+                        lhsT_scale=w_planes[:, w, channels],
+                        rhs=codes_of[j][:, rows].bitcast(FP8X4),
+                        rhs_scale=planes_of[j][:, rows],
+                        start=(source == 0),
+                        stop=(source == SOURCES - 1),
+                    )
+            return acc_t
+
+        def forget_sigmoids(j, acc_t):
+            forget_t = gates.tile([P, CHANNEL_TILES, P], F32)
             forget_t_of[j] = forget_t
             for m in range(CHANNEL_TILES):
-                nc.scalar.activation(
-                    out=forget_t[:, m, :],
-                    in_=banks[m // 2][:, m % 2, :],
-                    func=SIGMOID,
-                    bias=bias_f[:, m : m + 1],
-                )
+                nc.scalar.activation(out=forget_t[:, m, :], in_=acc_t[:, m, :], func=SIGMOID, bias=bias_f[:, m : m + 1])
 
         def forget_back(j):
-            for a in range(PAIR):
-                forget = psum.tile([P, D], F32)
-                forget_of[PAIR * j + a] = forget
-                for m in range(CHANNEL_TILES):
-                    nc.tensor.transpose(
-                        forget[:, m * P : (m + 1) * P],
-                        forget_t_of[j][:, m, a * P : (a + 1) * P],
-                        identity[:],
-                    )
+            forget = psum.tile([P, D], F32, bufs=1)
+            forget_of[j] = forget
+            for m in range(CHANNEL_TILES):
+                nc.tensor.transpose(forget[:, m * P : (m + 1) * P], forget_t_of[j][:, m, :], identity[:])
 
         def output_sums(j):
             accs = []
@@ -241,75 +247,73 @@ def tile_lstmmirrored_pb_t_kernel(
                     )
             return accs
 
+        def forget_bias(j, acc_f):
+            nc.vector.tensor_tensor(out=output_of[j][:, 0, :], in0=acc_f[:], in1=bias_f_all[:], op=ADD)
+
+        def new_sums(j):
+            sums = gates.tile([P, 1 + PAIR, D], F32)
+            output_of[j] = sums
+
         def output_bias(j, accs):
-            output = gates.tile([P, PAIR, D], F32)
-            output_of[j] = output
             for a in range(PAIR):
-                nc.vector.tensor_tensor(out=output[:, a, :], in0=accs[a][:], in1=bias_o[:], op=ADD)
+                nc.vector.tensor_tensor(out=output_of[j][:, 1 + a, :], in0=accs[a][:], in1=bias_o[:], op=ADD)
 
-        def output_sigmoid(j):
-            if j < PAIRS - 1:
-                both = output_of[j][:].rearrange("p a d -> p (a d)")
-                nc.scalar.activation(out=both, in_=both, func=SIGMOID)
-            else:
-                for a in range(PAIR):
-                    one = output_of[j][:, a, :]
-                    nc.scalar.activation(out=one, in_=one, func=SIGMOID)
+        def row_sigmoids(j, first, count):
+            some = output_of[j][:, first : first + count, :].rearrange("p s d -> p (s d)")
+            nc.scalar.activation(out=some, in_=some, func=SIGMOID)
 
-        def cell_and_hidden(j):
+        def new_results(j):
             c_out = results.tile([P, PAIR, D], F32)
             h_out = results.tile([P, PAIR, D], F32)
+            results_of[j] = (c_out, h_out)
+
+        def cell(j, a):
+            nc.vector.scalar_tensor_tensor(
+                out=results_of[j][0][:, a, :],
+                in0=forget_of[j][:] if a == 0 else output_of[j][:, 0, :],
+                scalar=gain[:],
+                in1=ig_of[PAIR * j + a],
+                op0=MULT,
+                op1=ADD,
+            )
+            if j >= PAIRS - 5:
+                nc.sync.dma_start(out=c_rows[:, PAIR * j + a, :], in_=results_of[j][0][:, a, :])
+
+        def hidden(j):
+            c_out, h_out = results_of[j]
             tiles = slice(PAIR * j, PAIR * (j + 1))
-
-            def cell(a):
-                nc.vector.scalar_tensor_tensor(
-                    out=c_out[:, a, :],
-                    in0=forget_of[PAIR * j + a][:],
-                    scalar=gain[:],
-                    in1=ig_of[PAIR * j + a],
-                    op0=MULT,
-                    op1=ADD,
-                )
-
-            def hidden(engine, a):
-                engine.tensor_tensor(out=h_out[:, a, :], in0=output_of[j][:, a, :], in1=c_out[:, a, :], op=MULT)
-
-            if j < PAIRS - 5:
-                for a in range(PAIR):
-                    cell(a)
-                    hidden(nc.gpsimd, a)
-                nc.sync.dma_start(out=c_rows[:, tiles, :], in_=c_out[:])
-                nc.sync.dma_start(out=h_rows[:, tiles, :], in_=h_out[:])
+            if j < PAIRS - LEAD - 1:
+                nc.gpsimd.tensor_tensor(out=h_out[:], in0=output_of[j][:, 1 : 1 + PAIR, :], in1=c_out[:], op=MULT)
             elif j < PAIRS - 1:
                 for a in range(PAIR):
-                    cell(a)
-                    hidden(nc.gpsimd, a)
-                    nc.sync.dma_start(out=c_rows[:, PAIR * j + a, :], in_=c_out[:, a, :])
-                for a in range(PAIR):
-                    nc.sync.dma_start(out=h_rows[:, PAIR * j + a, :], in_=h_out[:, a, :])
+                    nc.gpsimd.tensor_tensor(out=h_out[:, a, :], in0=output_of[j][:, 1 + a, :], in1=c_out[:, a, :], op=MULT)
+            if j < PAIRS - 5:
+                nc.sync.dma_start(out=c_rows[:, tiles, :], in_=c_out[:])
+                nc.sync.dma_start(out=h_rows[:, tiles, :], in_=h_out[:])
             else:
                 for a in range(PAIR):
-                    cell(a)
-                    nc.sync.dma_start(out=c_rows[:, PAIR * j + a, :], in_=c_out[:, a, :])
-                for a in range(PAIR):
-                    hidden(nc.vector, a)
+                    if j == PAIRS - 1:
+                        nc.vector.tensor_tensor(out=h_out[:, a, :], in0=output_of[j][:, 1 + a, :], in1=c_out[:, a, :], op=MULT)
                     nc.sync.dma_start(out=h_rows[:, PAIR * j + a, :], in_=h_out[:, a, :])
 
         def keep_warm(count):
             for i in range(count):
-                acc_t = psum.tile([P, 2, PAIR_ROWS], F32)
-                nc.tensor.matmul(out=acc_t[:].rearrange("p i r -> p (i r)"), lhsT=ones[:], rhs=zeros[:], start=True, stop=True)
+                acc_t = psum.tile([P, CHANNEL_TILES, P], F32, bufs=1)
+                nc.tensor.matmul(out=acc_t[:].rearrange("p m r -> p (m r)"), lhsT=ones[:], rhs=zeros[:], start=True, stop=True)
 
         def spread_bias_f():
             acc = psum.tile([P, D], F32)
             nc.tensor.transpose(acc[:, 0:P], bias_f_rows_f32[:], identity[:])
             nc.vector.tensor_copy(out=bias_f[:], in_=acc[:, 0:CHANNEL_TILES])
+            acc = psum.tile([P, D], F32)
+            nc.tensor.matmul(out=acc[:], lhsT=ones[:], rhs=bias_f_row[:], start=True, stop=True)
+            nc.vector.tensor_copy(out=bias_f_all[:], in_=acc[:])
 
         def spread_bias_o_and_gain():
-            forget = psum.tile([P, D], F32)
+            forget = psum.tile([P, D], F32, bufs=1)
             nc.tensor.matmul(out=forget[:], lhsT=ones[:], rhs=bias_o_rows[:], start=True, stop=True)
             nc.vector.tensor_copy(out=bias_o[:], in_=forget[:])
-            forget = psum.tile([P, D], F32)
+            forget = psum.tile([P, D], F32, bufs=1)
             nc.tensor.matmul(out=forget[:, 0:2], lhsT=ones[:], rhs=gain_rows[:], start=True, stop=True)
             nc.vector.tensor_copy(out=gain[:], in_=forget[:, 0:1])
 
@@ -329,16 +333,43 @@ def tile_lstmmirrored_pb_t_kernel(
                 regroup(j + LEAD, j == 0)
             if j >= 1:
                 forget_back(j - 1)
-                output_sigmoid(j - 1)
+                if j < PAIRS:
+                    row_sigmoids(j - 1, 0, 1 + PAIR)
             if j < PAIRS:
-                banks = forget_sums(j)
-                forget_sigmoids(j, banks)
-                accs = output_sums(j)
+                new_sums(j)
+                if last:
+                    acc_f = forget_sums_rows(j)
+                else:
+                    accs = output_sums(j)
+                acc_t = forget_sums_turned(j)
+                forget_sigmoids(j, acc_t)
+                if last:
+                    accs = output_sums(j)
+                else:
+                    acc_f = forget_sums_rows(j)
             if j == 0:
                 spread_bias_o_and_gain()
-            if j >= 1:
-                cell_and_hidden(j - 1)
-            if j + LEAD < PAIRS:
-                quantise(j + LEAD)
-            if j < PAIRS:
+            if 1 <= j < PAIRS:
+                new_results(j - 1)
+                cell(j - 1, 0)
+            if last:
+                forget_bias(j, acc_f)
+                row_sigmoids(j, 0, 1)
+                cell(j - 1, 1)
+                hidden(j - 1)
                 output_bias(j, accs)
+            elif j < PAIRS:
+                output_bias(j, accs)
+                if j + LEAD < PAIRS:
+                    quantise(j + LEAD)
+                if j >= 1:
+                    cell(j - 1, 1)
+                    hidden(j - 1)
+                forget_bias(j, acc_f)
+            else:
+                new_results(j - 1)
+                for a in range(PAIR):
+                    row_sigmoids(j - 1, 1 + a, 1)
+                cell(j - 1, 1)
+                cell(j - 1, 0)
+                hidden(j - 1)

@@ -77,8 +77,7 @@ def tile_lstmmirrored_pb_t_kernel(
         w_planes = const.tile([P, 2 * SOURCES, D], U8, align_bytes=64)
         bias_o_rows = const.tile([P, D], BF16)
         bias_o = const.tile([P, D], F32)
-        bias_f_rows = const.tile([P, P], BF16)
-        bias_f_rows_f32 = const.tile([P, P], F32)
+        bias_f_row_f32 = const.tile([P, D], F32)
         bias_f = const.tile([P, CHANNEL_TILES], F32)
         bias_f_row = const.tile([P, D], BF16)
         bias_f_all = const.tile([P, D], F32)
@@ -93,7 +92,6 @@ def tile_lstmmirrored_pb_t_kernel(
         nc.vector.memset(ones[:], 1.0)
         nc.vector.memset(zeros[:], 0.0)
         nc.vector.memset(table_warm[:], 0.0)
-        nc.vector.memset(bias_f_rows[:], 0.0)
         nc.vector.memset(bias_o_rows[:], 0.0)
         nc.vector.memset(bias_f_row[:], 0.0)
         nc.vector.memset(gain_rows[:], 0.0)
@@ -118,7 +116,6 @@ def tile_lstmmirrored_pb_t_kernel(
         first, count = chunks[2]
         load(nc.gpsimd, x_rows, x_of, "x", first, count)
         load(nc.gpsimd, hist_rows, hist_of, "hist", first, count)
-        nc.gpsimd.dma_start(out=bias_f_rows[0:CHANNEL_TILES, :], in_=b_f.rearrange("(m p) -> m p", p=P))
         nc.gpsimd.dma_start(out=bias_f_row[0:1, :], in_=b_f.rearrange("(e d) -> e d", e=1))
         nc.gpsimd.dma_start(out=bias_o_rows[0:1, :], in_=b_o.rearrange("(e d) -> e d", e=1))
         nc.gpsimd.dma_start(out=gain_rows[0:1, 0:1], in_=carousel.rearrange("(e d) -> e d", e=1))
@@ -198,15 +195,26 @@ def tile_lstmmirrored_pb_t_kernel(
                 )
             return acc_f
 
+        def mixed(j):
+            return j + LEAD < PAIRS
+
         def forget_sums_turned(j):
-            acc_t = psum.tile([P, CHANNEL_TILES, P], F32, bufs=1)
+            if mixed(j):
+                acc_t = psum.tile([P, CHANNEL_TILES, P], F32, bufs=1)
+                outs = [acc_t[:, m, :] for m in range(CHANNEL_TILES)]
+                count = P
+            else:
+                acc_t = psum.tile([P, 2, PAIR_ROWS], F32, bufs=1)
+                acc_f = psum.tile([P, 2, PAIR_ROWS], F32, bufs=1)
+                outs = [acc_t[:, 0, :], acc_t[:, 1, :], acc_f[:, 0, :], acc_f[:, 1, :]]
+                count = PAIR_ROWS
             for m in range(CHANNEL_TILES):
                 channels = slice(m * P, (m + 1) * P)
                 for source in range(SOURCES):
-                    rows = slice(source * PAIR_ROWS, source * PAIR_ROWS + P)
+                    rows = slice(source * PAIR_ROWS, source * PAIR_ROWS + count)
                     w = FORGET * SOURCES + source
                     nc.tensor.matmul_mx(
-                        out=acc_t[:, m, :],
+                        out=outs[m],
                         lhsT=w_words[:, w, channels].bitcast(FP8X4),
                         lhsT_scale=w_planes[:, w, channels],
                         rhs=codes_of[j][:, rows].bitcast(FP8X4),
@@ -214,19 +222,26 @@ def tile_lstmmirrored_pb_t_kernel(
                         start=(source == 0),
                         stop=(source == SOURCES - 1),
                     )
-            return acc_t
+            return outs
 
-        def forget_sigmoids(j, acc_t):
-            forget_t = gates.tile([P, CHANNEL_TILES, P], F32)
+        def forget_sigmoids(j, outs):
+            forget_t = gates.tile([P, CHANNEL_TILES, PAIR_ROWS], F32)
             forget_t_of[j] = forget_t
+            count = P if mixed(j) else PAIR_ROWS
             for m in range(CHANNEL_TILES):
-                nc.scalar.activation(out=forget_t[:, m, :], in_=acc_t[:, m, :], func=SIGMOID, bias=bias_f[:, m : m + 1])
+                nc.scalar.activation(out=forget_t[:, m, 0:count], in_=outs[m], func=SIGMOID, bias=bias_f[:, m : m + 1])
 
         def forget_back(j):
             forget = psum.tile([P, D], F32, bufs=1)
-            forget_of[j] = forget
-            for m in range(CHANNEL_TILES):
-                nc.tensor.transpose(forget[:, m * P : (m + 1) * P], forget_t_of[j][:, m, :], identity[:])
+            forget_of[j] = [forget]
+            if not mixed(j):
+                forget_b = psum.tile([P, D], F32, bufs=1)
+                forget_of[j].append(forget_b)
+            for a in range(len(forget_of[j])):
+                for m in range(CHANNEL_TILES):
+                    nc.tensor.transpose(
+                        forget_of[j][a][:, m * P : (m + 1) * P], forget_t_of[j][:, m, a * P : (a + 1) * P], identity[:]
+                    )
 
         def output_sums(j):
             accs = []
@@ -270,7 +285,7 @@ def tile_lstmmirrored_pb_t_kernel(
         def cell(j, a):
             nc.vector.scalar_tensor_tensor(
                 out=results_of[j][0][:, a, :],
-                in0=forget_of[j][:] if a == 0 else output_of[j][:, 0, :],
+                in0=forget_of[j][a][:] if a < len(forget_of[j]) else output_of[j][:, 0, :],
                 scalar=gain[:],
                 in1=ig_of[PAIR * j + a],
                 op0=MULT,
@@ -297,22 +312,27 @@ def tile_lstmmirrored_pb_t_kernel(
                     nc.sync.dma_start(out=h_rows[:, PAIR * j + a, :], in_=h_out[:, a, :])
 
         def keep_warm(count):
-            for i in range(count):
-                acc_t = psum.tile([P, CHANNEL_TILES, P], F32, bufs=1)
-                nc.tensor.matmul(out=acc_t[:].rearrange("p m r -> p (m r)"), lhsT=ones[:], rhs=zeros[:], start=True, stop=True)
+            for i in range(count // 2):
+                acc_t = psum.tile([P, D], F32, bufs=1)
+                nc.tensor.matmul(out=acc_t[:], lhsT=ones[:], rhs=zeros[:], start=True, stop=True)
+                acc_f = psum.tile([P, D], F32, bufs=1)
+                nc.tensor.matmul(out=acc_f[:], lhsT=ones[:], rhs=zeros[:], start=True, stop=True)
 
         def spread_bias_f():
             acc = psum.tile([P, D], F32)
-            nc.tensor.transpose(acc[:, 0:P], bias_f_rows_f32[:], identity[:])
-            nc.vector.tensor_copy(out=bias_f[:], in_=acc[:, 0:CHANNEL_TILES])
+            for m in range(CHANNEL_TILES):
+                nc.tensor.transpose(acc[:, m * P : (m + 1) * P], bias_f_row_f32[:, m * P : (m + 1) * P], identity[:])
+            nc.vector.tensor_copy(out=bias_f[:], in_=acc[:, 0:D:P])
             acc = psum.tile([P, D], F32)
             nc.tensor.matmul(out=acc[:], lhsT=ones[:], rhs=bias_f_row[:], start=True, stop=True)
             nc.vector.tensor_copy(out=bias_f_all[:], in_=acc[:])
 
-        def spread_bias_o_and_gain():
+        def spread_bias_o():
             forget = psum.tile([P, D], F32, bufs=1)
             nc.tensor.matmul(out=forget[:], lhsT=ones[:], rhs=bias_o_rows[:], start=True, stop=True)
             nc.vector.tensor_copy(out=bias_o[:], in_=forget[:])
+
+        def spread_gain():
             forget = psum.tile([P, D], F32, bufs=1)
             nc.tensor.matmul(out=forget[:, 0:2], lhsT=ones[:], rhs=gain_rows[:], start=True, stop=True)
             nc.vector.tensor_copy(out=gain[:], in_=forget[:, 0:1])
@@ -324,52 +344,45 @@ def tile_lstmmirrored_pb_t_kernel(
             regroup(j, True)
             quantise(j)
             if j == 1:
-                nc.vector.tensor_copy(out=bias_f_rows_f32[:], in_=bias_f_rows[:])
+                nc.vector.tensor_copy(out=bias_f_row_f32[:], in_=bias_f_row[:])
         spread_bias_f()
         for j in range(PAIRS + 1):
-            last = j == PAIRS - 1
             if j + LEAD < PAIRS:
                 transposes(j + LEAD)
                 regroup(j + LEAD, j == 0)
             if j >= 1:
                 forget_back(j - 1)
                 if j < PAIRS:
-                    row_sigmoids(j - 1, 0, 1 + PAIR)
+                    first = 0 if mixed(j - 1) else 1
+                    row_sigmoids(j - 1, first, 1 + PAIR - first)
+                else:
+                    for a in range(PAIR):
+                        row_sigmoids(j - 1, 1 + a, 1)
             if j < PAIRS:
                 new_sums(j)
-                if last:
+                if mixed(j):
+                    accs = output_sums(j)
+                    if j == 0:
+                        spread_bias_o()
+                    forget_sigmoids(j, forget_sums_turned(j))
                     acc_f = forget_sums_rows(j)
                 else:
+                    forget_sigmoids(j, forget_sums_turned(j))
                     accs = output_sums(j)
-                acc_t = forget_sums_turned(j)
-                forget_sigmoids(j, acc_t)
-                if last:
-                    accs = output_sums(j)
-                else:
-                    acc_f = forget_sums_rows(j)
             if j == 0:
-                spread_bias_o_and_gain()
-            if 1 <= j < PAIRS:
+                spread_gain()
+            if j >= 1:
                 new_results(j - 1)
                 cell(j - 1, 0)
-            if last:
-                forget_bias(j, acc_f)
-                row_sigmoids(j, 0, 1)
-                cell(j - 1, 1)
-                hidden(j - 1)
+            if j < PAIRS and mixed(j):
                 output_bias(j, accs)
-            elif j < PAIRS:
-                output_bias(j, accs)
-                if j + LEAD < PAIRS:
-                    quantise(j + LEAD)
+                quantise(j + LEAD)
                 if j >= 1:
                     cell(j - 1, 1)
                     hidden(j - 1)
                 forget_bias(j, acc_f)
             else:
-                new_results(j - 1)
-                for a in range(PAIR):
-                    row_sigmoids(j - 1, 1 + a, 1)
                 cell(j - 1, 1)
-                cell(j - 1, 0)
                 hidden(j - 1)
+                if j < PAIRS:
+                    output_bias(j, accs)

@@ -120,13 +120,14 @@ def tile_lstmmirrored_pb_t_kernel(
         nc.gpsimd.dma_start(out=bias_o_rows[0:1, :], in_=b_o.rearrange("(e d) -> e d", e=1))
         nc.gpsimd.dma_start(out=gain_rows[0:1, 0:1], in_=carousel.rearrange("(e d) -> e d", e=1))
 
-        for w in range(2 * SOURCES):
+        load_order = (OUTPUT * SOURCES, OUTPUT * SOURCES + 1, FORGET * SOURCES, FORGET * SOURCES + 1)
+        for w in load_order:
             for r in range(4):
                 nc.sync.dma_start(
                     out=w_planes[r:P:32, w, :].bitcast(I32),
                     in_=weight_scales[w][0, r:16:4, :].bitcast(I32),
                 )
-        for w in range(2 * SOURCES):
+        for w in load_order:
             nc.sync.dma_start(
                 out=w_words[:, w, :].bitcast(I32),
                 in_=weight_words[w][0].rearrange("p n t -> p (n t)").bitcast(I32),
@@ -147,10 +148,15 @@ def tile_lstmmirrored_pb_t_kernel(
         output_of = {}
         results_of = {}
 
-        def transposes(j):
+        def transposes(j, banks):
             turned_of[j] = []
-            for tile_of in (x_of, hist_of):
-                xt = psum.tile([P, 2, PAIR_ROWS], F32)
+            for source, tile_of in enumerate((x_of, hist_of)):
+                if banks == "own":
+                    xt = psum.tile([P, 2, PAIR_ROWS], F32)
+                elif banks == "output":
+                    xt = psum.tile([P, 2, PAIR_ROWS], F32, tag="acc")
+                else:
+                    xt = psum.tile([P, 2, PAIR_ROWS], F32, tag=("forget", "forget_b")[source], bufs=1)
                 turned_of[j].append(xt)
                 for a in range(PAIR):
                     words = tile_of[PAIR * j + a].bitcast(F32)
@@ -339,7 +345,7 @@ def tile_lstmmirrored_pb_t_kernel(
 
         keep_warm(4)
         for j in range(LEAD):
-            transposes(j)
+            transposes(j, ("own", "output", "forget")[j])
             keep_warm(2)
             regroup(j, True)
             quantise(j)
@@ -348,7 +354,7 @@ def tile_lstmmirrored_pb_t_kernel(
         spread_bias_f()
         for j in range(PAIRS + 1):
             if j + LEAD < PAIRS:
-                transposes(j + LEAD)
+                transposes(j + LEAD, "own")
                 regroup(j + LEAD, j == 0)
             if j >= 1:
                 forget_back(j - 1)

@@ -121,17 +121,18 @@ def tile_lstmmirrored_pb_t_kernel(
         nc.gpsimd.dma_start(out=gain_rows[0:1, 0:1], in_=carousel.rearrange("(e d) -> e d", e=1))
 
         load_order = (OUTPUT * SOURCES, OUTPUT * SOURCES + 1, FORGET * SOURCES, FORGET * SOURCES + 1)
-        for w in load_order:
-            for r in range(4):
+        for gate in range(2):
+            for w in load_order[SOURCES * gate : SOURCES * (gate + 1)]:
+                for r in range(4):
+                    nc.sync.dma_start(
+                        out=w_planes[r:P:32, w, :].bitcast(I32),
+                        in_=weight_scales[w][0, r:16:4, :].bitcast(I32),
+                    )
+            for w in load_order[SOURCES * gate : SOURCES * (gate + 1)]:
                 nc.sync.dma_start(
-                    out=w_planes[r:P:32, w, :].bitcast(I32),
-                    in_=weight_scales[w][0, r:16:4, :].bitcast(I32),
+                    out=w_words[:, w, :].bitcast(I32),
+                    in_=weight_words[w][0].rearrange("p n t -> p (n t)").bitcast(I32),
                 )
-        for w in load_order:
-            nc.sync.dma_start(
-                out=w_words[:, w, :].bitcast(I32),
-                in_=weight_words[w][0].rearrange("p n t -> p (n t)").bitcast(I32),
-            )
         for i in range(3, len(chunks) + IG_LAG):
             if i < len(chunks):
                 load(nc.sync, x_rows, x_of, "x", chunks[i][0], chunks[i][1])

from contextlib import ExitStack

import concourse.mybir as mybir
from concourse.masks import make_identity

F32 = mybir.dt.float32
BF16 = mybir.dt.bfloat16
I32 = mybir.dt.int32
U32 = mybir.dt.uint32
U8 = mybir.dt.uint8
FP8X4 = mybir.dt.float8_e4m3fn_x4
ADD = mybir.AluOpType.add
MULT = mybir.AluOpType.mult
SIGMOID = mybir.ActivationFunctionType.Sigmoid

P = 128
BATCH = 4096
D = 512
PACK = 4
ROW_TILES = BATCH // P
PAIR = 2
PAIRS = ROW_TILES // PAIR
PAIR_ROWS = PAIR * P
CHANNEL_TILES = D // P
MAX_CHUNK_TILES = 8
SOURCES = 2
FORGET = 0
OUTPUT = 1
LEAD = 3
IG_LAG = 2
OUT_BUFS = 8

FLOPS = 2 * BATCH * D * D * 2 * SOURCES


def tile_lstmmirrored_pb_t_kernel(
    tc,
    x,
    hist,
    ig,
    carousel,
    Wfx_words,
    Wfx_scales,
    Wfh_words,
    Wfh_scales,
    b_f,
    Wox_words,
    Wox_scales,
    Woh_words,
    Woh_scales,
    b_o,
    out_0,
    out_1,
):
    nc = tc.nc

    x_rows = x.rearrange("(p t) d -> p t d", t=ROW_TILES)
    hist_rows = hist.rearrange("(p t) d -> p t d", t=ROW_TILES)
    ig_rows = ig.rearrange("(p t) d -> p t d", t=ROW_TILES)
    h_rows = out_0.rearrange("(p t) d -> p t d", t=ROW_TILES)
    c_rows = out_1.rearrange("(p t) d -> p t d", t=ROW_TILES)

    weight_words = [Wfx_words, Wfh_words, Wox_words, Woh_words]
    weight_scales = [Wfx_scales, Wfh_scales, Wox_scales, Woh_scales]

    with ExitStack() as stack:
        const = stack.enter_context(tc.tile_pool(name="const", bufs=1))
        inputs = stack.enter_context(tc.tile_pool(name="inputs", bufs=1))
        staging = stack.enter_context(tc.tile_pool(name="staging", bufs=2))
        quant = stack.enter_context(tc.tile_pool(name="quant", bufs=LEAD + 2))
        gates = stack.enter_context(tc.tile_pool(name="gates", bufs=3))
        results = stack.enter_context(tc.tile_pool(name="results", bufs=OUT_BUFS))
        psum = stack.enter_context(tc.psum_pool(name="psum", bufs=2))
        stack.enter_context(tc.manual_schedule())

        w_words = const.tile([P, 2 * SOURCES, D], U32, align_bytes=64)
        w_planes = const.tile([P, 2 * SOURCES, D], U8, align_bytes=64)
        bias_o_rows = const.tile([P, D], BF16)
        bias_o = const.tile([P, D], F32)
        bias_f_row_f32 = const.tile([P, D], F32)
        bias_f = const.tile([P, CHANNEL_TILES], F32)
        bias_f_row = const.tile([P, D], BF16)
        bias_f_all = const.tile([P, D], F32)
        gain_rows = const.tile([P, 2], BF16)
        gain = const.tile([P, 1], F32)
        ones = const.tile([P, P], BF16)
        zeros = const.tile([P, D], BF16)
        table_warm = const.tile([P, 1], F32)
        identity = const.tile([P, P], F32)

        nc.vector.memset(w_planes[:].rearrange("p w n -> p (w n)").bitcast(I32), 0)
        nc.vector.memset(ones[:], 1.0)
        nc.vector.memset(zeros[:], 0.0)
        nc.vector.memset(table_warm[:], 0.0)
        nc.vector.memset(bias_o_rows[:], 0.0)
        nc.vector.memset(bias_f_row[:], 0.0)
        nc.vector.memset(gain_rows[:], 0.0)
        make_identity(nc, identity[:])

        chunks = [(0, 2), (2, 2), (4, 4), (8, 4), (12, 4), (16, 8), (24, 8)]

        x_of = {}
        hist_of = {}
        ig_of = {}

        def load(queue, rows, tile_of, name, first, count):
            chunk = inputs.tile([P, count, D], BF16, name="%s%d" % (name, first))
            queue.dma_start(out=chunk[:], in_=rows[:, first : first + count, :])
            for j in range(count):
                tile_of[first + j] = chunk[:, j, :]

        for first, count in chunks[:2]:
            load(nc.scalar, x_rows, x_of, "x", first, count)
            load(nc.scalar, hist_rows, hist_of, "hist", first, count)
        nc.scalar.activation(out=table_warm[:], in_=table_warm[:], func=SIGMOID)
        first, count = chunks[2]
        load(nc.gpsimd, x_rows, x_of, "x", first, count)
        load(nc.gpsimd, hist_rows, hist_of, "hist", first, count)
        nc.gpsimd.dma_start(out=bias_f_row[0:1, :], in_=b_f.rearrange("(e d) -> e d", e=1))
        nc.gpsimd.dma_start(out=bias_o_rows[0:1, :], in_=b_o.rearrange("(e d) -> e d", e=1))
        nc.gpsimd.dma_start(out=gain_rows[0:1, 0:1], in_=carousel.rearrange("(e d) -> e d", e=1))

        load_order = (OUTPUT * SOURCES, OUTPUT * SOURCES + 1, FORGET * SOURCES, FORGET * SOURCES + 1)
        for gate in range(2):
            for w in load_order[SOURCES * gate : SOURCES * (gate + 1)]:
                for r in range(4):
                    nc.sync.dma_start(
                        out=w_planes[r:P:32, w, :].bitcast(I32),
                        in_=weight_scales[w][0, r:16:4, :].bitcast(I32),
                    )
            for w in load_order[SOURCES * gate : SOURCES * (gate + 1)]:
                nc.sync.dma_start(
                    out=w_words[:, w, :].bitcast(I32),
                    in_=weight_words[w][0].rearrange("p n t -> p (n t)").bitcast(I32),
                )
        for i in range(3, len(chunks) + IG_LAG):
            if i < len(chunks):
                load(nc.sync, x_rows, x_of, "x", chunks[i][0], chunks[i][1])
                load(nc.sync, hist_rows, hist_of, "hist", chunks[i][0], chunks[i][1])
            for k in range(0 if i == 3 else i - IG_LAG, i - IG_LAG + 1):
                load(nc.sync, ig_rows, ig_of, "ig", chunks[k][0], chunks[k][1])

        turned_of = {}
        grouped_of = {}
        codes_of = {}
        planes_of = {}
        forget_t_of = {}
        forget_of = {}
        output_of = {}
        results_of = {}

        def transposes(j, banks):
            turned_of[j] = []
            for source, tile_of in enumerate((x_of, hist_of)):
                if banks == "own":
                    xt = psum.tile([P, 2, PAIR_ROWS], F32)
                elif banks == "output":
                    xt = psum.tile([P, 2, PAIR_ROWS], F32, tag="acc")
                else:
                    xt = psum.tile([P, 2, PAIR_ROWS], F32, tag=("forget", "forget_b")[source], bufs=1)
                turned_of[j].append(xt)
                for a in range(PAIR):
                    words = tile_of[PAIR * j + a].bitcast(F32)
                    for u in range(2):
                        nc.tensor.transpose(xt[:, u, a * P : (a + 1) * P], words[:, u : D // 2 : 2], identity[:])

        def regroup(j, hist_on_vector):
            grouped = staging.tile([P, SOURCES, PAIR_ROWS * PACK], BF16, align_bytes=64)
            grouped_of[j] = grouped
            for source in range(SOURCES):
                out = grouped[:, source, :].bitcast(F32).rearrange("p (r u) -> p r u", u=2)
                in_ = turned_of[j][source][:].rearrange("p u r -> p r u")
                if source == 1 and hist_on_vector:
                    nc.vector.tensor_copy(out=out, in_=in_)
                else:
                    nc.scalar.copy(out=out, in_=in_)

        def quantise(j):
            codes = quant.tile([P, SOURCES * PAIR_ROWS], U32, align_bytes=64)
            planes = quant.tile([P, SOURCES * PAIR_ROWS], U8, align_bytes=64)
            codes_of[j] = codes
            planes_of[j] = planes
            nc.vector.quantize_mx(
                out=codes[:].bitcast(FP8X4),
                scales=planes[:],
                in_=grouped_of[j][:].rearrange("p s c -> p (s c)"),
            )

        def forget_sums_rows(j):
            acc_f = psum.tile([P, D], F32, bufs=1)
            for source in range(SOURCES):
                rows = slice(source * PAIR_ROWS + P, source * PAIR_ROWS + 2 * P)
                w = FORGET * SOURCES + source
                nc.tensor.matmul_mx(
                    out=acc_f[:],
                    lhsT=codes_of[j][:, rows].bitcast(FP8X4),
                    lhsT_scale=planes_of[j][:, rows],
                    rhs=w_words[:, w, :].bitcast(FP8X4),
                    rhs_scale=w_planes[:, w, :],
                    start=(source == 0),
                    stop=(source == SOURCES - 1),
                )
            return acc_f

        def mixed(j):
            return j + LEAD < PAIRS

        def forget_sums_turned(j):
            if mixed(j):
                acc_t = psum.tile([P, CHANNEL_TILES, P], F32, bufs=1)
                outs = [acc_t[:, m, :] for m in range(CHANNEL_TILES)]
                count = P
            else:
                acc_t = psum.tile([P, 2, PAIR_ROWS], F32, bufs=1)
                acc_f = psum.tile([P, 2, PAIR_ROWS], F32, bufs=1)
                outs = [acc_t[:, 0, :], acc_t[:, 1, :], acc_f[:, 0, :], acc_f[:, 1, :]]
                count = PAIR_ROWS
            for m in range(CHANNEL_TILES):
                channels = slice(m * P, (m + 1) * P)
                for source in range(SOURCES):
                    rows = slice(source * PAIR_ROWS, source * PAIR_ROWS + count)
                    w = FORGET * SOURCES + source
                    nc.tensor.matmul_mx(
                        out=outs[m],
                        lhsT=w_words[:, w, channels].bitcast(FP8X4),
                        lhsT_scale=w_planes[:, w, channels],
                        rhs=codes_of[j][:, rows].bitcast(FP8X4),
                        rhs_scale=planes_of[j][:, rows],
                        start=(source == 0),
                        stop=(source == SOURCES - 1),
                    )
            return outs

        def forget_sigmoids(j, outs):
            forget_t = gates.tile([P, CHANNEL_TILES, PAIR_ROWS], F32)
            forget_t_of[j] = forget_t
            count = P if mixed(j) else PAIR_ROWS
            for m in range(CHANNEL_TILES):
                nc.scalar.activation(out=forget_t[:, m, 0:count], in_=outs[m], func=SIGMOID, bias=bias_f[:, m : m + 1])

        def forget_back(j):
            forget = psum.tile([P, D], F32, bufs=1)
            forget_of[j] = [forget]
            if not mixed(j):
                forget_b = psum.tile([P, D], F32, bufs=1)
                forget_of[j].append(forget_b)
            for a in range(len(forget_of[j])):
                for m in range(CHANNEL_TILES):
                    nc.tensor.transpose(
                        forget_of[j][a][:, m * P : (m + 1) * P], forget_t_of[j][:, m, a * P : (a + 1) * P], identity[:]
                    )

        def output_sums(j):
            accs = []
            for a in range(PAIR):
                acc = psum.tile([P, D], F32)
                accs.append(acc)
                for source in range(SOURCES):
                    rows = slice(source * PAIR_ROWS + a * P, source * PAIR_ROWS + (a + 1) * P)
                    w = OUTPUT * SOURCES + source
                    nc.tensor.matmul_mx(
                        out=acc[:],
                        lhsT=codes_of[j][:, rows].bitcast(FP8X4),
                        lhsT_scale=planes_of[j][:, rows],
                        rhs=w_words[:, w, :].bitcast(FP8X4),
                        rhs_scale=w_planes[:, w, :],
                        start=(source == 0),
                        stop=(source == SOURCES - 1),
                    )
            return accs

        def forget_bias(j, acc_f):
            nc.vector.tensor_tensor(out=output_of[j][:, 0, :], in0=acc_f[:], in1=bias_f_all[:], op=ADD)

        def new_sums(j):
            sums = gates.tile([P, 1 + PAIR, D], F32)
            output_of[j] = sums

        def output_bias(j, accs):
            for a in range(PAIR):
                nc.vector.tensor_tensor(out=output_of[j][:, 1 + a, :], in0=accs[a][:], in1=bias_o[:], op=ADD)

        def row_sigmoids(j, first, count):
            some = output_of[j][:, first : first + count, :].rearrange("p s d -> p (s d)")
            nc.scalar.activation(out=some, in_=some, func=SIGMOID)

        def new_results(j):
            c_out = results.tile([P, PAIR, D], F32)
            h_out = results.tile([P, PAIR, D], F32)
            results_of[j] = (c_out, h_out)

        def cell(j, a):
            nc.vector.scalar_tensor_tensor(
                out=results_of[j][0][:, a, :],
                in0=forget_of[j][a][:] if a < len(forget_of[j]) else output_of[j][:, 0, :],
                scalar=gain[:],
                in1=ig_of[PAIR * j + a],
                op0=MULT,
                op1=ADD,
            )
            if j >= PAIRS - 5:
                nc.sync.dma_start(out=c_rows[:, PAIR * j + a, :], in_=results_of[j][0][:, a, :])

        def hidden(j):
            c_out, h_out = results_of[j]
            tiles = slice(PAIR * j, PAIR * (j + 1))
            if j < PAIRS - LEAD - 1:
                nc.gpsimd.tensor_tensor(out=h_out[:], in0=output_of[j][:, 1 : 1 + PAIR, :], in1=c_out[:], op=MULT)
            elif j < PAIRS - 1:
                for a in range(PAIR):
                    nc.gpsimd.tensor_tensor(out=h_out[:, a, :], in0=output_of[j][:, 1 + a, :], in1=c_out[:, a, :], op=MULT)
            if j < PAIRS - 5:
                nc.sync.dma_start(out=c_rows[:, tiles, :], in_=c_out[:])
                nc.sync.dma_start(out=h_rows[:, tiles, :], in_=h_out[:])
            else:
                for a in range(PAIR):
                    if j == PAIRS - 1:
                        nc.vector.tensor_tensor(out=h_out[:, a, :], in0=output_of[j][:, 1 + a, :], in1=c_out[:, a, :], op=MULT)
                    nc.sync.dma_start(out=h_rows[:, PAIR * j + a, :], in_=h_out[:, a, :])

        def keep_warm(count):
            for i in range(count // 2):
                acc_t = psum.tile([P, D], F32, bufs=1)
                nc.tensor.matmul(out=acc_t[:], lhsT=ones[:], rhs=zeros[:], start=True, stop=True)
                acc_f = psum.tile([P, D], F32, bufs=1)
                nc.tensor.matmul(out=acc_f[:], lhsT=ones[:], rhs=zeros[:], start=True, stop=True)

        def spread_bias_f():
            acc = psum.tile([P, D], F32)
            for m in range(CHANNEL_TILES):
                nc.tensor.transpose(acc[:, m * P : (m + 1) * P], bias_f_row_f32[:, m * P : (m + 1) * P], identity[:])
            nc.vector.tensor_copy(out=bias_f[:], in_=acc[:, 0:D:P])
            acc = psum.tile([P, D], F32)
            nc.tensor.matmul(out=acc[:], lhsT=ones[:], rhs=bias_f_row[:], start=True, stop=True)
            nc.vector.tensor_copy(out=bias_f_all[:], in_=acc[:])

        def spread_bias_o():
            forget = psum.tile([P, D], F32, bufs=1)
            nc.tensor.matmul(out=forget[:], lhsT=ones[:], rhs=bias_o_rows[:], start=True, stop=True)
            nc.vector.tensor_copy(out=bias_o[:], in_=forget[:])

        def spread_gain():
            forget = psum.tile([P, D], F32, bufs=1)
            nc.tensor.matmul(out=forget[:, 0:2], lhsT=ones[:], rhs=gain_rows[:], start=True, stop=True)
            nc.vector.tensor_copy(out=gain[:], in_=forget[:, 0:1])

        keep_warm(4)
        for j in range(LEAD):
            transposes(j, ("own", "output", "forget")[j])
            keep_warm(2)
            regroup(j, True)
            quantise(j)
            if j == 1:
                nc.vector.tensor_copy(out=bias_f_row_f32[:], in_=bias_f_row[:])
        spread_bias_f()
        for j in range(PAIRS + 1):
            if j + LEAD < PAIRS:
                transposes(j + LEAD, "own")
                regroup(j + LEAD, j == 0)
            if j >= 1:
                forget_back(j - 1)
                if j < PAIRS:
                    first = 0 if mixed(j - 1) else 1
                    row_sigmoids(j - 1, first, 1 + PAIR - first)
                else:
                    for a in range(PAIR):
                        row_sigmoids(j - 1, 1 + a, 1)
            if j < PAIRS:
                new_sums(j)
                if mixed(j):
                    accs = output_sums(j)
                    if j == 0:
                        spread_bias_o()
                    forget_sigmoids(j, forget_sums_turned(j))
                    acc_f = forget_sums_rows(j)
                else:
                    forget_sigmoids(j, forget_sums_turned(j))
                    accs = output_sums(j)
            if j == 0:
                spread_gain()
            if j >= 1:
                new_results(j - 1)
                cell(j - 1, 0)
            if j < PAIRS and mixed(j):
                output_bias(j, accs)
                quantise(j + LEAD)
                if j >= 1:
                    cell(j - 1, 1)
                    hidden(j - 1)
                forget_bias(j, acc_f)
            else:
                cell(j - 1, 1)
                hidden(j - 1)
                if j < PAIRS:
                    output_bias(j, accs)
